import numpy as np
import ml_dtypes


def mxq(x, axis, fmt="e4m3"):
    dtype, down = {"e4m3": (ml_dtypes.float8_e4m3fn, 7), "e5m2": (ml_dtypes.float8_e5m2, 14)}[fmt]
    v = np.moveaxis(np.asarray(x, np.float32).astype(ml_dtypes.bfloat16).astype(np.float64), axis, -1)
    blocks = v.reshape(v.shape[:-1] + (-1, 32))
    amax = np.abs(blocks).max(-1, keepdims=True)
    byte = np.maximum(np.where(amax > 0, np.frexp(amax)[1] - 1 + 127, 0) - down, 1)
    scale = np.exp2(byte - 127.0)
    codes = (blocks / scale).astype(np.float32).astype(dtype).astype(np.float64)
    return np.moveaxis((codes * scale).reshape(v.shape), -1, axis)


WIDE = False


def mx_kscale(k):
    if not WIDE:
        return np.ones(k)
    levels = np.array([10, -10, 5, -5, 0])
    if k % 512:
        return np.exp2(np.random.permutation(np.resize(levels, k // 32))).repeat(32)
    a = np.empty((k // 512, 16))
    for p in range(k // 512):
        a[p, :8] = np.random.permutation(np.resize(levels, 8))
        for g in range(8):
            far = levels[np.abs(levels - a[p, g]) >= 10]
            a[p, g + 8] = far[np.random.randint(len(far))]
    return np.exp2(a.ravel()).repeat(32)


BF16 = ml_dtypes.bfloat16


def bf(x):
    return np.asarray(x, np.float32).astype(BF16)


def f64(x):
    return np.asarray(x).astype(np.float64)


B, S, A, O, H, L = 1024, 1024, 128, 1920, 1024, 384
K1 = S + A + O


def setup_inputs():
    s = mx_kscale(K1)
    t = mx_kscale(H)
    col = np.concatenate([np.full(L, 0.7), np.full(L, 0.14)]) / np.sqrt(H)
    return {"prev_state": bf(np.random.standard_normal((B, S)) * s[:S]),
            "prev_action": bf(np.random.standard_normal((B, A)) * s[S:S + A]),
            "observation": bf(np.random.standard_normal((B, O)) * s[S + A:]),
            "eps": bf(np.random.standard_normal((B, L))),
            "rep_W1": bf(np.random.standard_normal((K1, H)) / np.sqrt(K1) / s[:, None] * t),
            "rep_b1": bf(np.random.standard_normal(H) * 0.1 * t),
            "rep_W2": bf(np.random.standard_normal((H, 2 * L)) * col / t[:, None]),
            "rep_b2": bf(np.concatenate([0.1 * np.random.standard_normal(L), 1.0 + 0.1 * np.random.standard_normal(L)]))}


def reference(prev_state, prev_action, observation, eps, rep_W1, rep_b1, rep_W2, rep_b2):
    x = np.concatenate([f64(prev_state), f64(prev_action), f64(observation)], axis=-1)
    h1 = np.maximum((mxq(x, 1, "e4m3") @ mxq(f64(rep_W1), 0, "e4m3")) + f64(rep_b1), 0.0)
    out = (mxq(h1, 1, "e4m3") @ mxq(f64(rep_W2), 0, "e4m3")) + f64(rep_b2)
    mean, std = np.split(out, 2, axis=-1)
    sample = mean + np.sqrt(std) * f64(eps)
    return mean, std, sample

@@ -1,0 +1,343 @@
+from contextlib import ExitStack
+
+import concourse.mybir as mybir
+from concourse.masks import make_identity
+
+F32 = mybir.dt.float32
+BF16 = mybir.dt.bfloat16
+U32 = mybir.dt.uint32
+U8 = mybir.dt.uint8
+FP8X4 = mybir.dt.float8_e4m3fn_x4
+ACT = mybir.ActivationFunctionType
+ALU = mybir.AluOpType
+
+P = 128
+PACK = 4
+K_PASS = P * PACK
+
+BATCH, STATE, ACTION, OBS, HIDDEN, LATENT = 1024, 1024, 128, 1920, 1024, 384
+K1 = STATE + ACTION + OBS
+OUT = 2 * LATENT
+PASSES1 = K1 // K_PASS
+PASSES2 = HIDDEN // K_PASS
+
+HALF = 512
+HALVES = BATCH // HALF
+QUARTER = HALF // 2
+SUB = HALF // P
+X_CHUNK = 2 * K_PASS
+CHUNKS = K1 // X_CHUNK
+WORDS = K_PASS // 2
+
+H_TILES = HIDDEN // P
+LOW = (0, 1, 2, 3)
+HIGH = (4, 5, 6, 7)
+RUN = 8
+W_BUFS = 4
+
+OUT_BANKS = ((0, HALF), (HALF, OUT))
+
+VECTOR_SHARE_16THS = 8
+
+FLOPS = 2 * BATCH * K1 * HIDDEN + 2 * BATCH * HIDDEN * OUT
+
+
+def tile_rssm_pa_kernel(
+    tc, prev_state, prev_action, observation, eps, rep_W1, rep_b1, rep_W2, rep_b2, out_0, out_1, out_2
+):
+    nc = tc.nc
+    with ExitStack() as ctx:
+        keep = ctx.enter_context(tc.tile_pool(name="keep", bufs=1))
+        x_raw_pool = ctx.enter_context(tc.tile_pool(name="x_raw", bufs=3))
+        x_grp_pool = ctx.enter_context(tc.tile_pool(name="x_grp", bufs=4))
+        w_raw_pool = ctx.enter_context(tc.tile_pool(name="w_raw", bufs=W_BUFS))
+        w_grp_pool = ctx.enter_context(tc.tile_pool(name="w_grp", bufs=2))
+        hidden_pool = ctx.enter_context(tc.tile_pool(name="hidden", bufs=2))
+        result_pool = ctx.enter_context(tc.tile_pool(name="result", bufs=3))
+        psum = ctx.enter_context(tc.psum_pool(name="psum", bufs=4))
+
+        def by_tile(dram):
+            return dram.rearrange("(h p t) c -> h p t c", h=HALVES, t=SUB)
+
+        x_sources = ((by_tile(prev_state), 0), (by_tile(prev_action), STATE), (by_tile(observation), STATE + ACTION))
+        outputs = (by_tile(out_0), by_tile(out_1), by_tile(out_2))
+
+        x_codes = keep.tile([P, HALVES, PASSES1, HALF], U32, align_bytes=64)
+        x_scales = keep.tile([P, HALVES, PASSES1, HALF], U8, align_bytes=64)
+        w1_codes = keep.tile([P, PASSES1, HIDDEN], U32, align_bytes=64)
+        w1_scales = keep.tile([P, PASSES1, HIDDEN], U8, align_bytes=64)
+        h1_codes = keep.tile([P, PASSES2, BATCH], U32, align_bytes=64)
+        h1_scales = keep.tile([P, PASSES2, BATCH], U8, align_bytes=64)
+        w2_codes = keep.tile([P, PASSES2, OUT], U32, align_bytes=64)
+        w2_scales = keep.tile([P, PASSES2, OUT], U8, align_bytes=64)
+
+        def load_x(half, chunk):
+            raw = x_raw_pool.tile([P, SUB * X_CHUNK], BF16, name="x_raw")
+            rows = raw[:].rearrange("p (t k) -> p t k", t=SUB)
+            first = chunk * X_CHUNK
+            for source, start in x_sources:
+                lo = max(start, first)
+                hi = min(start + source.shape[3], first + X_CHUNK)
+                if lo < hi:
+                    nc.sync.dma_start(out=rows[:, :, lo - first : hi - first], in_=source[half, :, :, lo - start : hi - start])
+            return raw
+
+        def load_w1(g):
+            raw = w_raw_pool.tile([P, PACK, HIDDEN], BF16, name="w1_raw", tag="w_raw")
+            nc.sync.dma_start(out=raw[:], in_=rep_W1[g * K_PASS : (g + 1) * K_PASS, :].rearrange("(p j) w -> p j w", j=PACK))
+            return raw
+
+        def load_w2(g):
+            raw = w_raw_pool.tile([P, PACK, OUT], BF16, name="w2_raw", tag="w_raw")
+            rows = rep_W2[g * K_PASS : (g + 1) * K_PASS, :].rearrange("(b t i) n -> t b i n", t=PACK, i=RUN)
+            for t in range(PACK):
+                nc.sync.dma_start(out=raw[:, t, :], in_=rows[t])
+            return raw
+
+        def transpose_chunk(raw, bank_set):
+            words = raw[:].bitcast(F32)
+            banks = []
+            for local in range(X_CHUNK // K_PASS):
+                for pair in range(SUB // 2):
+                    bank = psum.tile([P, 2, 2 * P], F32, name="x_bank", tag=bank_set)
+                    for u in range(2):
+                        for tt in range(2):
+                            first = (2 * pair + tt) * (X_CHUNK // 2) + local * WORDS
+                            nc.tensor.transpose(
+                                out=bank[:, u, tt * P : (tt + 1) * P], in_=words[:, first + u : first + WORDS : 2], identity=ident[:]
+                            )
+                    banks.append(bank)
+            grouped_tiles = []
+            for local in range(X_CHUNK // K_PASS):
+                grouped = x_grp_pool.tile([P, HALF * PACK], BF16, name="x_grp", align_bytes=64)
+                word_pairs = grouped[:].bitcast(F32).rearrange("p (c u) -> p c u", u=2)
+                for pair in range(SUB // 2):
+                    nc.scalar.copy(
+                        out=word_pairs[:, pair * 2 * P : (pair + 1) * 2 * P, :],
+                        in_=banks[local * (SUB // 2) + pair][:].rearrange("p u c -> p c u"),
+                    )
+                grouped_tiles.append(grouped)
+            return grouped_tiles
+
+        def quantise_x(half, g, grouped):
+            nc.vector.quantize_mx(out=x_codes[:, half, g, :].bitcast(FP8X4), scales=x_scales[:, half, g, :], in_=grouped[:])
+
+        def group_rows(copy, grouped, raw, cols):
+            copy(
+                out=grouped[:, cols, :].rearrange("p (c i) t -> p c t i", i=4),
+                in_=raw[:, :, cols].rearrange("p t (c i) -> p c t i", i=4),
+            )
+
+        def group_weight(raw, width):
+            grouped = w_grp_pool.tile([P, width, PACK], BF16, name="w_grp", tag="w_grp", align_bytes=64)
+            split = width * VECTOR_SHARE_16THS // 16
+            group_rows(nc.vector.tensor_copy, grouped, raw, slice(0, split))
+            group_rows(nc.scalar.copy, grouped, raw, slice(split, width))
+            return grouped
+
+        def group_w1(raw):
+            grouped = w_grp_pool.tile([P, HIDDEN, PACK], BF16, name="w_grp", tag="w_grp", align_bytes=64)
+            source = raw[:].rearrange("p j (b t i) -> p t b j i", t=PACK, i=RUN)
+            target = grouped[:].rearrange("p (t b i) j -> p t b j i", t=PACK, i=RUN)
+            for t, copy in ((0, nc.vector.tensor_copy), (2, nc.scalar.copy), (1, nc.vector.tensor_copy), (3, nc.scalar.copy)):
+                copy(out=target[:, t], in_=source[:, t])
+            return grouped
+
+        def quantise_weight(codes, scales, grouped, cols):
+            nc.vector.quantize_mx(
+                out=codes[:, cols].bitcast(FP8X4),
+                scales=scales[:, cols],
+                in_=grouped[:, cols, :].rearrange("p w t -> p (w t)"),
+            )
+
+        def open_groups(h_tiles, bank_set, width):
+            for h in h_tiles:
+                acc[h] = psum.tile([P, width], F32, name="acc", tag=bank_set)
+
+        def first_product(half, h_tiles, passes, cols):
+            for g in passes:
+                for h in h_tiles:
+                    first = (h % PACK) * PASSES2 * P + (h // PACK) * P
+                    nc.tensor.matmul_mx(
+                        out=acc[h][:],
+                        lhsT=w1_codes[:, g, first : first + P].bitcast(FP8X4),
+                        lhsT_scale=w1_scales[:, g, first : first + P],
+                        rhs=x_codes[:, half, g, cols].bitcast(FP8X4),
+                        rhs_scale=x_scales[:, half, g, cols],
+                        start=(g == 0),
+                        stop=(g == PASSES1 - 1),
+                    )
+
+        def relu_out(hidden, h, on_vector):
+            if on_vector:
+                nc.vector.tensor_scalar(
+                    out=hidden[:, h % PACK, :], in0=acc[h][:], scalar1=b1_col[:, h : h + 1], scalar2=0.0, op0=ALU.add, op1=ALU.max
+                )
+            else:
+                nc.scalar.activation(out=hidden[:, h % PACK, :], in_=acc[h][:], func=ACT.Relu, bias=b1_col[:, h : h + 1], scale=1.0)
+
+        def group_hidden(hidden, width):
+            grouped = hidden_pool.tile([P, width, PACK], BF16, name="h1_grp", align_bytes=64)
+            group_rows(nc.vector.tensor_copy, grouped, hidden, slice(0, width))
+            return grouped
+
+        def quantise_hidden(g, first_row, width, grouped):
+            cols = slice(first_row, first_row + width)
+            nc.vector.quantize_mx(
+                out=h1_codes[:, g, cols].bitcast(FP8X4), scales=h1_scales[:, g, cols], in_=grouped[:].rearrange("p c t -> p (c t)")
+            )
+
+        def second_product(half, t, bank_set):
+            rows = slice(half * HALF + t * P, half * HALF + (t + 1) * P)
+            result = result_pool.tile([P, OUT], F32, name="result")
+            for first, last in OUT_BANKS:
+                cols = slice(first, last)
+                bank = psum.tile([P, last - first], F32, name="out_bank", tag=bank_set)
+                for g in range(PASSES2):
+                    nc.tensor.matmul_mx(
+                        out=bank[:],
+                        lhsT=h1_codes[:, g, rows].bitcast(FP8X4),
+                        lhsT_scale=h1_scales[:, g, rows],
+                        rhs=w2_codes[:, g, cols].bitcast(FP8X4),
+                        rhs_scale=w2_scales[:, g, cols],
+                        start=(g == 0),
+                        stop=(g == PASSES2 - 1),
+                    )
+                nc.vector.tensor_tensor(out=result[:, cols], in0=bank[:], in1=b2_all[:, cols], op=ALU.add)
+            root = result_pool.tile([P, LATENT], F32, name="root")
+            nc.scalar.activation(out=root[:], in_=result[:, LATENT:OUT], func=ACT.Sqrt)
+            nc.sync.dma_start(out=outputs[0][half, :, t, :], in_=result[:, 0:LATENT])
+            nc.sync.dma_start(out=outputs[1][half, :, t, :], in_=result[:, LATENT:OUT])
+            return result, root
+
+        def draw_sample(half, t, result, root):
+            noise = result_pool.tile([P, LATENT], F32, name="noise")
+            nc.vector.tensor_tensor(out=noise[:], in0=root[:], in1=eps_all[:, half, t, :], op=ALU.mult)
+            sample = result_pool.tile([P, LATENT], F32, name="sample")
+            nc.gpsimd.tensor_tensor(out=sample[:], in0=noise[:], in1=result[:, 0:LATENT], op=ALU.add)
+            nc.sync.dma_start(out=outputs[2][half, :, t, :], in_=sample[:])
+
+        def finish_half(half, bank_set):
+            waiting = None
+            for t in range(SUB):
+                fresh = second_product(half, t, bank_set)
+                if waiting is not None:
+                    draw_sample(half, t - 1, waiting[0], waiting[1])
+                waiting = fresh
+            draw_sample(half, SUB - 1, waiting[0], waiting[1])
+
+        ident = keep.tile([P, P], F32)
+        make_identity(nc, ident[:])
+        b1_rows = keep.tile([P, P], BF16)
+        nc.vector.memset(b1_rows[:], 0.0)
+        b1_runs = rep_b1.rearrange("(q b t i) -> q t b i", q=PASSES2, t=PACK, i=RUN)
+        for q in range(PASSES2):
+            nc.sync.dma_start(out=b1_rows[PACK * q : PACK * (q + 1), :].rearrange("t (b i) -> t b i", i=RUN), in_=b1_runs[q])
+        b2_row = keep.tile([P, OUT], BF16)
+        nc.vector.memset(b2_row[:], 0.0)
+        nc.sync.dma_start(out=b2_row[0:1, :], in_=rep_b2.rearrange("(o n) -> o n", o=1))
+        ones = keep.tile([P, P], BF16)
+        nc.vector.memset(ones[:], 1.0)
+        one = keep.tile([P, 1], F32)
+        nc.vector.memset(one[:], 1.0)
+        one_root = keep.tile([P, 1], F32)
+        nc.scalar.activation(out=one_root[:], in_=one[:], func=ACT.Sqrt)
+
+        x_raw = {}
+        w_raw = {}
+        for chunk in range(CHUNKS):
+            x_raw[(0, chunk)] = load_x(0, chunk)
+        for g in range(W_BUFS):
+            w_raw[g] = load_w1(g)
+
+        b1_rows_f32 = keep.tile([P, P], F32)
+        nc.vector.tensor_copy(out=b1_rows_f32[:], in_=b1_rows[:])
+        b1_bank = psum.tile([P, P], F32, tag="y")
+        nc.tensor.transpose(out=b1_bank[:], in_=b1_rows_f32[:], identity=ident[:])
+        b1_col = keep.tile([P, H_TILES], F32)
+        nc.vector.tensor_copy(out=b1_col[:], in_=b1_bank[:, 0:H_TILES])
+        b2_all = keep.tile([P, OUT], F32)
+        for first, last in OUT_BANKS:
+            cols = slice(first, last)
+            b2_bank = psum.tile([P, last - first], F32, name="b2_bank", tag="y")
+            nc.tensor.matmul(out=b2_bank[:], lhsT=ones[:], rhs=b2_row[:, cols], start=True, stop=True)
+            nc.vector.tensor_copy(out=b2_all[:, cols], in_=b2_bank[:])
+
+        def leave_psum(h_tiles, share_with_vector):
+            hidden = hidden_pool.tile([P, PACK, HALF], BF16, name="hidden")
+            for h in h_tiles:
+                relu_out(hidden, h, share_with_vector and h % 2 == 1)
+            return hidden
+
+        whole = slice(0, HALF)
+
+        acc = {}
+        grouped_w = {}
+        waiting = None
+        for chunk in range(CHUNKS):
+            fresh = transpose_chunk(x_raw[(0, chunk)], ("y", "x")[chunk % 2])
+            if waiting is not None:
+                quantise_x(0, 2 * chunk - 2, waiting[0])
+                quantise_x(0, 2 * chunk - 1, waiting[1])
+            waiting = fresh
+        quantise_x(0, 2 * CHUNKS - 2, waiting[0])
+        quantise_x(0, 2 * CHUNKS - 1, waiting[1])
+
+        open_groups(LOW, "x", HALF)
+        open_groups(HIGH, "y", HALF)
+        w2_raw = []
+        for g in range(PASSES1 + 1):
+            if g > 0:
+                quantise_weight(w1_codes[:, g - 1, :], w1_scales[:, g - 1, :], grouped_w[g - 1], slice(0, HIDDEN))
+                first_product(0, LOW + HIGH, (g - 1,), whole)
+            if g < PASSES1:
+                grouped_w[g] = group_w1(w_raw[g])
+            if g + W_BUFS < PASSES1:
+                w_raw[g + W_BUFS] = load_w1(g + W_BUFS)
+            elif g + W_BUFS < PASSES1 + PASSES2:
+                w2_raw.append(load_w2(g + W_BUFS - PASSES1))
+        for chunk in range(CHUNKS):
+            x_raw[(1, chunk)] = load_x(1, chunk)
+        eps_all = keep.tile([P, HALVES, SUB, LATENT], BF16)
+        nc.sync.dma_start(out=eps_all[:], in_=eps.rearrange("(h p t) c -> p h t c", h=HALVES, t=SUB))
+
+        for g in range(PASSES2):
+            grouped_w[g] = group_weight(w2_raw[g], OUT)
+        hidden_low = leave_psum(LOW, True)
+        hidden_high = leave_psum(HIGH, True)
+        for g in range(PASSES2):
+            for first, last in OUT_BANKS:
+                quantise_weight(w2_codes[:, g, :], w2_scales[:, g, :], grouped_w[g], slice(first, last))
+
+        grouped_x = transpose_chunk(x_raw[(1, 0)], "x") + transpose_chunk(x_raw[(1, 1)], "x")
+        quantise_x(1, 0, grouped_x[0])
+        grouped_h = group_hidden(hidden_low, HALF)
+        quantise_x(1, 1, grouped_x[1])
+        quantise_hidden(0, 0, HALF, grouped_h)
+        open_groups(LOW, "y", HALF)
+        first_product(1, LOW, (0, 1), whole)
+        grouped_x = grouped_x + transpose_chunk(x_raw[(1, 2)], "x")
+        quantise_x(1, 2, grouped_x[2])
+        grouped_h = group_hidden(hidden_high, HALF)
+        quantise_x(1, 3, grouped_x[3])
+        quantise_hidden(1, 0, HALF, grouped_h)
+        first_product(1, LOW, (2, 3), whole)
+        quantise_x(1, 4, grouped_x[4])
+        quantise_x(1, 5, grouped_x[5])
+        finish_half(0, "x")
+        first_product(1, LOW, (4, 5), whole)
+        hidden_low = leave_psum(LOW, False)
+
+        grouped_q = {}
+        for quarter, bank_set in enumerate(("y", "x")):
+            hidden_high = hidden_pool.tile([P, PACK, QUARTER], BF16, name="hidden_q")
+            for h in HIGH:
+                open_groups((h,), bank_set, QUARTER)
+                first_product(1, (h,), range(PASSES1), slice(quarter * QUARTER, (quarter + 1) * QUARTER))
+                relu_out(hidden_high, h, False)
+            if quarter == 0:
+                grouped_h = group_hidden(hidden_low, HALF)
+                quantise_hidden(0, HALF, HALF, grouped_h)
+            grouped_q[quarter] = group_hidden(hidden_high, QUARTER)
+            quantise_hidden(1, HALF + quarter * QUARTER, QUARTER, grouped_q[quarter])
+        finish_half(1, "y")

@@ -10,6 +10,7 @@ U8 = mybir.dt.uint8
 FP8X4 = mybir.dt.float8_e4m3fn_x4
 ACT = mybir.ActivationFunctionType
 ALU = mybir.AluOpType
+PE = mybir.EngineType.PE
 
 P = 128
 PACK = 4
@@ -29,15 +30,13 @@ X_CHUNK = 2 * K_PASS
 CHUNKS = K1 // X_CHUNK
 WORDS = K_PASS // 2
 
+W_BUFS = 7
+RUN = 8
 H_TILES = HIDDEN // P
 LOW = (0, 1, 2, 3)
 HIGH = (4, 5, 6, 7)
-RUN = 8
-W_BUFS = 4
 
-OUT_BANKS = ((0, HALF), (HALF, OUT))
-
-VECTOR_SHARE_16THS = 8
+OUT_BANKS = ((OUT - HALF, OUT), (0, OUT - HALF))
 
 FLOPS = 2 * BATCH * K1 * HIDDEN + 2 * BATCH * HIDDEN * OUT
 
@@ -48,13 +47,14 @@ def tile_rssm_pa_kernel(
     nc = tc.nc
     with ExitStack() as ctx:
         keep = ctx.enter_context(tc.tile_pool(name="keep", bufs=1))
-        x_raw_pool = ctx.enter_context(tc.tile_pool(name="x_raw", bufs=3))
+        x_raw_pool = ctx.enter_context(tc.tile_pool(name="x_raw", bufs=4))
         x_grp_pool = ctx.enter_context(tc.tile_pool(name="x_grp", bufs=4))
         w_raw_pool = ctx.enter_context(tc.tile_pool(name="w_raw", bufs=W_BUFS))
-        w_grp_pool = ctx.enter_context(tc.tile_pool(name="w_grp", bufs=2))
+        w_grp_pool = ctx.enter_context(tc.tile_pool(name="w_grp", bufs=3))
         hidden_pool = ctx.enter_context(tc.tile_pool(name="hidden", bufs=2))
         result_pool = ctx.enter_context(tc.tile_pool(name="result", bufs=3))
         psum = ctx.enter_context(tc.psum_pool(name="psum", bufs=4))
+        ctx.enter_context(tc.manual_schedule(engines={PE}))
 
         def by_tile(dram):
             return dram.rearrange("(h p t) c -> h p t c", h=HALVES, t=SUB)
@@ -71,52 +71,60 @@ def tile_rssm_pa_kernel(
         w2_codes = keep.tile([P, PASSES2, OUT], U32, align_bytes=64)
         w2_scales = keep.tile([P, PASSES2, OUT], U8, align_bytes=64)
 
-        def load_x(half, chunk):
-            raw = x_raw_pool.tile([P, SUB * X_CHUNK], BF16, name="x_raw")
+        def new_x():
+            return x_raw_pool.tile([P, SUB * X_CHUNK], BF16, name="x_raw")
+
+        def fill_x(raw, half, chunk, tiles):
             rows = raw[:].rearrange("p (t k) -> p t k", t=SUB)
             first = chunk * X_CHUNK
             for source, start in x_sources:
                 lo = max(start, first)
                 hi = min(start + source.shape[3], first + X_CHUNK)
                 if lo < hi:
-                    nc.sync.dma_start(out=rows[:, :, lo - first : hi - first], in_=source[half, :, :, lo - start : hi - start])
+                    nc.sync.dma_start(out=rows[:, tiles, lo - first : hi - first], in_=source[half, :, tiles, lo - start : hi - start])
+
+        def load_x(half, chunk):
+            raw = new_x()
+            fill_x(raw, half, chunk, slice(0, SUB))
             return raw
 
-        def load_w1(g):
-            raw = w_raw_pool.tile([P, PACK, HIDDEN], BF16, name="w1_raw", tag="w_raw")
-            nc.sync.dma_start(out=raw[:], in_=rep_W1[g * K_PASS : (g + 1) * K_PASS, :].rearrange("(p j) w -> p j w", j=PACK))
+        def load_w1(q, g):
+            raw = w_raw_pool.tile([P, PACK, K_PASS], BF16, name="w1_raw", tag="w_raw", bufs=W_BUFS)
+            rows = rep_W1[g * K_PASS : (g + 1) * K_PASS, q * K_PASS : (q + 1) * K_PASS]
+            nc.sync.dma_start(out=raw[:], in_=rows.rearrange("(p j) w -> p j w", j=PACK))
             return raw
 
         def load_w2(g):
-            raw = w_raw_pool.tile([P, PACK, OUT], BF16, name="w2_raw", tag="w_raw")
+            raw = w_raw_pool.tile([P, PACK, OUT], BF16, name="w2_raw", tag="w2_raw", bufs=PASSES2)
             rows = rep_W2[g * K_PASS : (g + 1) * K_PASS, :].rearrange("(b t i) n -> t b i n", t=PACK, i=RUN)
             for t in range(PACK):
                 nc.sync.dma_start(out=raw[:, t, :], in_=rows[t])
             return raw
 
-        def transpose_chunk(raw, bank_set):
+        def transpose_chunk(raw, bank_set, vector_banks=()):
             words = raw[:].bitcast(F32)
-            banks = []
-            for local in range(X_CHUNK // K_PASS):
-                for pair in range(SUB // 2):
+            banks = {}
+            for pair in range(SUB // 2):
+                for local in range(X_CHUNK // K_PASS):
                     bank = psum.tile([P, 2, 2 * P], F32, name="x_bank", tag=bank_set)
-                    for u in range(2):
-                        for tt in range(2):
+                    for tt in range(2):
+                        for u in range(2):
                             first = (2 * pair + tt) * (X_CHUNK // 2) + local * WORDS
                             nc.tensor.transpose(
                                 out=bank[:, u, tt * P : (tt + 1) * P], in_=words[:, first + u : first + WORDS : 2], identity=ident[:]
                             )
-                    banks.append(bank)
+                    banks[local, pair] = bank
             grouped_tiles = []
             for local in range(X_CHUNK // K_PASS):
-                grouped = x_grp_pool.tile([P, HALF * PACK], BF16, name="x_grp", align_bytes=64)
-                word_pairs = grouped[:].bitcast(F32).rearrange("p (c u) -> p c u", u=2)
-                for pair in range(SUB // 2):
-                    nc.scalar.copy(
+                grouped_tiles.append(x_grp_pool.tile([P, HALF * PACK], BF16, name="x_grp", align_bytes=64))
+            for pair in range(SUB // 2):
+                for local in range(X_CHUNK // K_PASS):
+                    word_pairs = grouped_tiles[local][:].bitcast(F32).rearrange("p (c u) -> p c u", u=2)
+                    copy = nc.vector.tensor_copy if (pair, local) in vector_banks else nc.scalar.copy
+                    copy(
                         out=word_pairs[:, pair * 2 * P : (pair + 1) * 2 * P, :],
-                        in_=banks[local * (SUB // 2) + pair][:].rearrange("p u c -> p c u"),
+                        in_=banks[local, pair][:].rearrange("p u c -> p c u"),
                     )
-                grouped_tiles.append(grouped)
             return grouped_tiles
 
         def quantise_x(half, g, grouped):
@@ -128,19 +136,19 @@ def tile_rssm_pa_kernel(
                 in_=raw[:, :, cols].rearrange("p t (c i) -> p c t i", i=4),
             )
 
-        def group_weight(raw, width):
-            grouped = w_grp_pool.tile([P, width, PACK], BF16, name="w_grp", tag="w_grp", align_bytes=64)
-            split = width * VECTOR_SHARE_16THS // 16
-            group_rows(nc.vector.tensor_copy, grouped, raw, slice(0, split))
-            group_rows(nc.scalar.copy, grouped, raw, slice(split, width))
+        def group_w1(raw, vector_tiles):
+            grouped = w_grp_pool.tile([P, K_PASS, PACK], BF16, name="w_grp", align_bytes=64)
+            target = grouped[:].rearrange("p (t b i) j -> p t b j i", t=PACK, i=RUN)
+            source = raw[:].rearrange("p j (b t i) -> p t b j i", t=PACK, i=RUN)
+            nc.vector.tensor_copy(out=target[:, 0:vector_tiles], in_=source[:, 0:vector_tiles])
+            for t in range(vector_tiles, PACK):
+                nc.scalar.copy(out=target[:, t], in_=source[:, t])
             return grouped
 
-        def group_w1(raw):
-            grouped = w_grp_pool.tile([P, HIDDEN, PACK], BF16, name="w_grp", tag="w_grp", align_bytes=64)
-            source = raw[:].rearrange("p j (b t i) -> p t b j i", t=PACK, i=RUN)
-            target = grouped[:].rearrange("p (t b i) j -> p t b j i", t=PACK, i=RUN)
-            for t, copy in ((0, nc.vector.tensor_copy), (2, nc.scalar.copy), (1, nc.vector.tensor_copy), (3, nc.scalar.copy)):
-                copy(out=target[:, t], in_=source[:, t])
+        def group_w2(raw):
+            grouped = w_grp_pool.tile([P, OUT, PACK], BF16, name="w2_grp", align_bytes=64, bufs=2)
+            group_rows(nc.vector.tensor_copy, grouped, raw, slice(0, OUT // 2))
+            group_rows(nc.scalar.copy, grouped, raw, slice(OUT // 2, OUT))
             return grouped
 
         def quantise_weight(codes, scales, grouped, cols):
@@ -157,7 +165,7 @@ def tile_rssm_pa_kernel(
         def first_product(half, h_tiles, passes, cols):
             for g in passes:
                 for h in h_tiles:
-                    first = (h % PACK) * PASSES2 * P + (h // PACK) * P
+                    first = h * P
                     nc.tensor.matmul_mx(
                         out=acc[h][:],
                         lhsT=w1_codes[:, g, first : first + P].bitcast(FP8X4),
@@ -176,6 +184,12 @@ def tile_rssm_pa_kernel(
             else:
                 nc.scalar.activation(out=hidden[:, h % PACK, :], in_=acc[h][:], func=ACT.Relu, bias=b1_col[:, h : h + 1], scale=1.0)
 
+        def leave_psum(h_tiles, vector_tiles):
+            hidden = hidden_pool.tile([P, PACK, HALF], BF16, name="hidden")
+            for h in h_tiles:
+                relu_out(hidden, h, h in vector_tiles)
+            return hidden
+
         def group_hidden(hidden, width):
             grouped = hidden_pool.tile([P, width, PACK], BF16, name="h1_grp", align_bytes=64)
             group_rows(nc.vector.tensor_copy, grouped, hidden, slice(0, width))
@@ -189,7 +203,7 @@ def tile_rssm_pa_kernel(
 
         def second_product(half, t, bank_set):
             rows = slice(half * HALF + t * P, half * HALF + (t + 1) * P)
-            result = result_pool.tile([P, OUT], F32, name="result")
+            result = w_raw_pool.tile([P, OUT], F32, name="result", tag="w_raw", bufs=W_BUFS)
             for first, last in OUT_BANKS:
                 cols = slice(first, last)
                 bank = psum.tile([P, last - first], F32, name="out_bank", tag=bank_set)
@@ -206,8 +220,8 @@ def tile_rssm_pa_kernel(
                 nc.vector.tensor_tensor(out=result[:, cols], in0=bank[:], in1=b2_all[:, cols], op=ALU.add)
             root = result_pool.tile([P, LATENT], F32, name="root")
             nc.scalar.activation(out=root[:], in_=result[:, LATENT:OUT], func=ACT.Sqrt)
-            nc.sync.dma_start(out=outputs[0][half, :, t, :], in_=result[:, 0:LATENT])
             nc.sync.dma_start(out=outputs[1][half, :, t, :], in_=result[:, LATENT:OUT])
+            nc.sync.dma_start(out=outputs[0][half, :, t, :], in_=result[:, 0:LATENT])
             return result, root
 
         def draw_sample(half, t, result, root):
@@ -226,8 +240,6 @@ def tile_rssm_pa_kernel(
                 waiting = fresh
             draw_sample(half, SUB - 1, waiting[0], waiting[1])
 
-        ident = keep.tile([P, P], F32)
-        make_identity(nc, ident[:])
         b1_rows = keep.tile([P, P], BF16)
         nc.vector.memset(b1_rows[:], 0.0)
         b1_runs = rep_b1.rearrange("(q b t i) -> q t b i", q=PASSES2, t=PACK, i=RUN)
@@ -236,6 +248,26 @@ def tile_rssm_pa_kernel(
         b2_row = keep.tile([P, OUT], BF16)
         nc.vector.memset(b2_row[:], 0.0)
         nc.sync.dma_start(out=b2_row[0:1, :], in_=rep_b2.rearrange("(o n) -> o n", o=1))
+
+        x_raw = {}
+        w_raw = {}
+        w_raw[0, 0] = load_w1(0, 0)
+        x_raw[0, 0] = new_x()
+        fill_x(x_raw[0, 0], 0, 0, slice(0, SUB // 2))
+        fill_x(x_raw[0, 0], 0, 0, slice(SUB // 2, SUB))
+        w_raw[0, 1] = load_w1(0, 1)
+        x_raw[0, 1] = load_x(0, 1)
+        for g in (2, 3):
+            w_raw[0, g] = load_w1(0, g)
+        x_raw[0, 2] = load_x(0, 2)
+        for g in (4, 5):
+            w_raw[0, g] = load_w1(0, g)
+        x_raw[1, 0] = load_x(1, 0)
+        w_raw[1, 0] = load_w1(1, 0)
+        w_raw[1, 1] = load_w1(1, 1)
+
+        ident = keep.tile([P, P], F32)
+        make_identity(nc, ident[:])
         ones = keep.tile([P, P], BF16)
         nc.vector.memset(ones[:], 1.0)
         one = keep.tile([P, 1], F32)
@@ -243,13 +275,29 @@ def tile_rssm_pa_kernel(
         one_root = keep.tile([P, 1], F32)
         nc.scalar.activation(out=one_root[:], in_=one[:], func=ACT.Sqrt)
 
-        x_raw = {}
-        w_raw = {}
-        for chunk in range(CHUNKS):
-            x_raw[(0, chunk)] = load_x(0, chunk)
-        for g in range(W_BUFS):
-            w_raw[g] = load_w1(g)
+        whole = slice(0, HALF)
+        acc = {}
+        grouped_w = {}
 
+        grouped_x = {}
+
+        def x_ready(half, chunk):
+            quantise_x(half, 2 * chunk, grouped_x[half, chunk][0])
+            quantise_x(half, 2 * chunk + 1, grouped_x[half, chunk][1])
+
+        def weight_pass(q, g, vector_tiles=2):
+            grouped_w[q, g] = group_w1(w_raw[q, g], vector_tiles)
+
+        def weight_ready(q, g):
+            cols = slice(q * K_PASS, (q + 1) * K_PASS)
+            nc.vector.quantize_mx(
+                out=w1_codes[:, g, cols].bitcast(FP8X4),
+                scales=w1_scales[:, g, cols],
+                in_=grouped_w[q, g][:].rearrange("p w t -> p (w t)"),
+            )
+
+        weight_pass(0, 0)
+        grouped_x[0, 0] = transpose_chunk(x_raw[0, 0], "x", ((0, 1), (1, 1)))
         b1_rows_f32 = keep.tile([P, P], F32)
         nc.vector.tensor_copy(out=b1_rows_f32[:], in_=b1_rows[:])
         b1_bank = psum.tile([P, P], F32, tag="y")
@@ -261,83 +309,94 @@ def tile_rssm_pa_kernel(
             cols = slice(first, last)
             b2_bank = psum.tile([P, last - first], F32, name="b2_bank", tag="y")
             nc.tensor.matmul(out=b2_bank[:], lhsT=ones[:], rhs=b2_row[:, cols], start=True, stop=True)
-            nc.vector.tensor_copy(out=b2_all[:, cols], in_=b2_bank[:])
+            nc.scalar.copy(out=b2_all[:, cols], in_=b2_bank[:])
 
-        def leave_psum(h_tiles, share_with_vector):
-            hidden = hidden_pool.tile([P, PACK, HALF], BF16, name="hidden")
-            for h in h_tiles:
-                relu_out(hidden, h, share_with_vector and h % 2 == 1)
-            return hidden
-
-        whole = slice(0, HALF)
-
-        acc = {}
-        grouped_w = {}
-        waiting = None
-        for chunk in range(CHUNKS):
-            fresh = transpose_chunk(x_raw[(0, chunk)], ("y", "x")[chunk % 2])
-            if waiting is not None:
-                quantise_x(0, 2 * chunk - 2, waiting[0])
-                quantise_x(0, 2 * chunk - 1, waiting[1])
-            waiting = fresh
-        quantise_x(0, 2 * CHUNKS - 2, waiting[0])
-        quantise_x(0, 2 * CHUNKS - 1, waiting[1])
-
-        open_groups(LOW, "x", HALF)
-        open_groups(HIGH, "y", HALF)
-        w2_raw = []
-        for g in range(PASSES1 + 1):
-            if g > 0:
-                quantise_weight(w1_codes[:, g - 1, :], w1_scales[:, g - 1, :], grouped_w[g - 1], slice(0, HIDDEN))
-                first_product(0, LOW + HIGH, (g - 1,), whole)
-            if g < PASSES1:
-                grouped_w[g] = group_w1(w_raw[g])
-            if g + W_BUFS < PASSES1:
-                w_raw[g + W_BUFS] = load_w1(g + W_BUFS)
-            elif g + W_BUFS < PASSES1 + PASSES2:
-                w2_raw.append(load_w2(g + W_BUFS - PASSES1))
-        for chunk in range(CHUNKS):
-            x_raw[(1, chunk)] = load_x(1, chunk)
+        weight_ready(0, 0)
+        weight_pass(0, 1)
+        x_ready(0, 0)
+        grouped_x[0, 1] = transpose_chunk(x_raw[0, 1], "x", ((1, 1),))
+        weight_ready(0, 1)
+        open_groups(LOW, "y", HALF)
+        first_product(0, LOW, (0, 1), whole)
+        weight_pass(0, 2)
+        x_ready(0, 1)
+        grouped_x[0, 2] = transpose_chunk(x_raw[0, 2], "x", ((1, 1),))
+        weight_ready(0, 2)
+        weight_pass(0, 3)
+        weight_ready(0, 3)
+        first_product(0, LOW, (2, 3), whole)
+        weight_pass(0, 4)
+        x_ready(0, 2)
+        weight_ready(0, 4)
+        grouped_x[1, 0] = transpose_chunk(x_raw[1, 0], "x", ((1, 1),))
+        weight_pass(0, 5)
+        weight_ready(0, 5)
+        first_product(0, LOW, (4, 5), whole)
+        x_raw[1, 1] = load_x(1, 1)
+        w_raw[1, 2] = load_w1(1, 2)
+        w_raw[1, 3] = load_w1(1, 3)
+        x_raw[1, 2] = load_x(1, 2)
+        w_raw[1, 4] = load_w1(1, 4)
+        w_raw[1, 5] = load_w1(1, 5)
+        w2_raw = [load_w2(0), load_w2(1)]
         eps_all = keep.tile([P, HALVES, SUB, LATENT], BF16)
         nc.sync.dma_start(out=eps_all[:], in_=eps.rearrange("(h p t) c -> p h t c", h=HALVES, t=SUB))
 
+        hidden_low = leave_psum(LOW, (1,))
+        x_ready(1, 0)
+        grouped_x[1, 1] = transpose_chunk(x_raw[1, 1], "x", ((1, 1),))
+        open_groups(LOW, "y", HALF)
+        first_product(1, LOW, (0, 1), whole)
+        x_ready(1, 1)
+        weight_pass(1, 0)
+        weight_ready(1, 0)
+        grouped_x[1, 2] = transpose_chunk(x_raw[1, 2], "x", ((1, 1),))
+        first_product(1, LOW, (2, 3), whole)
+        weight_pass(1, 1)
+        x_ready(1, 2)
+        weight_ready(1, 1)
+
+        open_groups(HIGH, "x", HALF)
+        first_product(0, HIGH, (0,), whole)
+        first_product(1, LOW, (4, 5), whole)
+        for g in (2, 3):
+            weight_pass(1, g)
+            first_product(0, HIGH, (g - 1,), whole)
+            weight_ready(1, g)
+        grouped_h = group_hidden(hidden_low, HALF)
+        hidden_low = leave_psum(LOW, ())
+        quantise_hidden(0, 0, HALF, grouped_h)
+        for g in (4, 5):
+            weight_pass(1, g)
+            first_product(0, HIGH, (g - 1,), whole)
+            weight_ready(1, g)
+        first_product(0, HIGH, (5,), whole)
+        hidden_high = leave_psum(HIGH, (5, 7))
         for g in range(PASSES2):
-            grouped_w[g] = group_weight(w2_raw[g], OUT)
-        hidden_low = leave_psum(LOW, True)
-        hidden_high = leave_psum(HIGH, True)
+            grouped_w[g] = group_w2(w2_raw[g])
+        grouped_l = group_hidden(hidden_low, HALF)
         for g in range(PASSES2):
             for first, last in OUT_BANKS:
                 quantise_weight(w2_codes[:, g, :], w2_scales[:, g, :], grouped_w[g], slice(first, last))
-
-        grouped_x = transpose_chunk(x_raw[(1, 0)], "x") + transpose_chunk(x_raw[(1, 1)], "x")
-        quantise_x(1, 0, grouped_x[0])
-        grouped_h = group_hidden(hidden_low, HALF)
-        quantise_x(1, 1, grouped_x[1])
-        quantise_hidden(0, 0, HALF, grouped_h)
-        open_groups(LOW, "y", HALF)
-        first_product(1, LOW, (0, 1), whole)
-        grouped_x = grouped_x + transpose_chunk(x_raw[(1, 2)], "x")
-        quantise_x(1, 2, grouped_x[2])
         grouped_h = group_hidden(hidden_high, HALF)
-        quantise_x(1, 3, grouped_x[3])
+        quantise_hidden(0, HALF, HALF, grouped_l)
         quantise_hidden(1, 0, HALF, grouped_h)
-        first_product(1, LOW, (2, 3), whole)
-        quantise_x(1, 4, grouped_x[4])
-        quantise_x(1, 5, grouped_x[5])
-        finish_half(0, "x")
-        first_product(1, LOW, (4, 5), whole)
-        hidden_low = leave_psum(LOW, False)
 
-        grouped_q = {}
-        for quarter, bank_set in enumerate(("y", "x")):
-            hidden_high = hidden_pool.tile([P, PACK, QUARTER], BF16, name="hidden_q")
+        def last_tiles(quarter, bank_set):
+            hidden = hidden_pool.tile([P, PACK, QUARTER], BF16, name="hidden_q")
             for h in HIGH:
                 open_groups((h,), bank_set, QUARTER)
                 first_product(1, (h,), range(PASSES1), slice(quarter * QUARTER, (quarter + 1) * QUARTER))
-                relu_out(hidden_high, h, False)
-            if quarter == 0:
-                grouped_h = group_hidden(hidden_low, HALF)
-                quantise_hidden(0, HALF, HALF, grouped_h)
-            grouped_q[quarter] = group_hidden(hidden_high, QUARTER)
-            quantise_hidden(1, HALF + quarter * QUARTER, QUARTER, grouped_q[quarter])
-        finish_half(1, "y")
+                relu_out(hidden, h, False)
+            return hidden
+
+        def last_hidden(quarter, hidden):
+            grouped = group_hidden(hidden, QUARTER)
+            quantise_hidden(1, HALF + quarter * QUARTER, QUARTER, grouped)
+
+        hidden_q = last_tiles(0, "y")
+        last_hidden(0, hidden_q)
+        finish_half(0, "x")
+        hidden_q = last_tiles(1, "y")
+        last_hidden(1, hidden_q)
+        finish_half(1, "x")

@@ -30,7 +30,7 @@ X_CHUNK = 2 * K_PASS
 CHUNKS = K1 // X_CHUNK
 WORDS = K_PASS // 2
 
-W_BUFS = 7
+W_BUFS = 6
 RUN = 8
 H_TILES = HIDDEN // P
 LOW = (0, 1, 2, 3)
@@ -52,7 +52,7 @@ def tile_rssm_pa_kernel(
         w_raw_pool = ctx.enter_context(tc.tile_pool(name="w_raw", bufs=W_BUFS))
         w_grp_pool = ctx.enter_context(tc.tile_pool(name="w_grp", bufs=3))
         hidden_pool = ctx.enter_context(tc.tile_pool(name="hidden", bufs=2))
-        result_pool = ctx.enter_context(tc.tile_pool(name="result", bufs=3))
+        result_pool = ctx.enter_context(tc.tile_pool(name="result", bufs=4))
         psum = ctx.enter_context(tc.psum_pool(name="psum", bufs=4))
         ctx.enter_context(tc.manual_schedule(engines={PE}))
 
@@ -190,9 +190,12 @@ def tile_rssm_pa_kernel(
                 relu_out(hidden, h, h in vector_tiles)
             return hidden
 
-        def group_hidden(hidden, width):
+        def group_hidden(hidden, width, vector_cols):
             grouped = hidden_pool.tile([P, width, PACK], BF16, name="h1_grp", align_bytes=64)
-            group_rows(nc.vector.tensor_copy, grouped, hidden, slice(0, width))
+            if vector_cols > 0:
+                group_rows(nc.vector.tensor_copy, grouped, hidden, slice(0, vector_cols))
+            if vector_cols < width:
+                group_rows(nc.scalar.copy, grouped, hidden, slice(vector_cols, width))
             return grouped
 
         def quantise_hidden(g, first_row, width, grouped):
@@ -228,48 +231,57 @@ def tile_rssm_pa_kernel(
             noise = result_pool.tile([P, LATENT], F32, name="noise")
             nc.vector.tensor_tensor(out=noise[:], in0=root[:], in1=eps_all[:, half, t, :], op=ALU.mult)
             sample = result_pool.tile([P, LATENT], F32, name="sample")
-            nc.gpsimd.tensor_tensor(out=sample[:], in0=noise[:], in1=result[:, 0:LATENT], op=ALU.add)
+            sum_engine = nc.vector if half == 1 and t == SUB - 1 else nc.gpsimd
+            sum_engine.tensor_tensor(out=sample[:], in0=noise[:], in1=result[:, 0:LATENT], op=ALU.add)
             nc.sync.dma_start(out=outputs[2][half, :, t, :], in_=sample[:])
 
-        def finish_half(half, bank_set):
-            waiting = None
-            for t in range(SUB):
-                fresh = second_product(half, t, bank_set)
-                if waiting is not None:
-                    draw_sample(half, t - 1, waiting[0], waiting[1])
-                waiting = fresh
-            draw_sample(half, SUB - 1, waiting[0], waiting[1])
+        waiting = []
 
+        def finish_tile(half, t, bank_set):
+            result, root = second_product(half, t, bank_set)
+            if waiting:
+                draw_sample(*waiting.pop())
+            waiting.append((half, t, result, root))
+
+        ones = keep.tile([P, P], BF16)
+        nc.vector.memset(ones[:], 1.0)
         b1_rows = keep.tile([P, P], BF16)
         nc.vector.memset(b1_rows[:], 0.0)
-        b1_runs = rep_b1.rearrange("(q b t i) -> q t b i", q=PASSES2, t=PACK, i=RUN)
-        for q in range(PASSES2):
-            nc.sync.dma_start(out=b1_rows[PACK * q : PACK * (q + 1), :].rearrange("t (b i) -> t b i", i=RUN), in_=b1_runs[q])
         b2_row = keep.tile([P, OUT], BF16)
         nc.vector.memset(b2_row[:], 0.0)
-        nc.sync.dma_start(out=b2_row[0:1, :], in_=rep_b2.rearrange("(o n) -> o n", o=1))
 
         x_raw = {}
         w_raw = {}
-        w_raw[0, 0] = load_w1(0, 0)
         x_raw[0, 0] = new_x()
         fill_x(x_raw[0, 0], 0, 0, slice(0, SUB // 2))
         fill_x(x_raw[0, 0], 0, 0, slice(SUB // 2, SUB))
-        w_raw[0, 1] = load_w1(0, 1)
+        w_raw[0, 0] = load_w1(0, 0)
         x_raw[0, 1] = load_x(0, 1)
-        for g in (2, 3):
-            w_raw[0, g] = load_w1(0, g)
+        w_raw[0, 1] = load_w1(0, 1)
+        w_raw[0, 2] = load_w1(0, 2)
+        b1_runs = rep_b1.rearrange("(q b t i) -> q t b i", q=PASSES2, t=PACK, i=RUN)
+        for q in range(PASSES2):
+            nc.sync.dma_start(out=b1_rows[PACK * q : PACK * (q + 1), :].rearrange("t (b i) -> t b i", i=RUN), in_=b1_runs[q])
+        nc.sync.dma_start(out=b2_row[0:1, :], in_=rep_b2.rearrange("(o n) -> o n", o=1))
         x_raw[0, 2] = load_x(0, 2)
-        for g in (4, 5):
-            w_raw[0, g] = load_w1(0, g)
+        w_raw[0, 3] = load_w1(0, 3)
+        w_raw[0, 4] = load_w1(0, 4)
         x_raw[1, 0] = load_x(1, 0)
+        w_raw[0, 5] = load_w1(0, 5)
+        x_raw[1, 1] = load_x(1, 1)
+        x_raw[1, 2] = load_x(1, 2)
         w_raw[1, 0] = load_w1(1, 0)
         w_raw[1, 1] = load_w1(1, 1)
+        w_raw[1, 2] = load_w1(1, 2)
+        w_raw[1, 3] = load_w1(1, 3)
+        w_raw[1, 4] = load_w1(1, 4)
+        w_raw[1, 5] = load_w1(1, 5)
+        w2_raw = [load_w2(0), load_w2(1)]
+        eps_all = keep.tile([P, HALVES, SUB, LATENT], BF16)
+        nc.sync.dma_start(out=eps_all[:], in_=eps.rearrange("(h p t) c -> p h t c", h=HALVES, t=SUB))
 
         ident = keep.tile([P, P], F32)
         make_identity(nc, ident[:])
-        ones = keep.tile([P, P], BF16)
-        nc.vector.memset(ones[:], 1.0)
         one = keep.tile([P, 1], F32)
         nc.vector.memset(one[:], 1.0)
         one_root = keep.tile([P, 1], F32)
@@ -298,6 +310,10 @@ def tile_rssm_pa_kernel(
 
         weight_pass(0, 0)
         grouped_x[0, 0] = transpose_chunk(x_raw[0, 0], "x", ((0, 1), (1, 1)))
+        weight_ready(0, 0)
+        weight_pass(0, 1)
+        x_ready(0, 0)
+        grouped_x[0, 1] = transpose_chunk(x_raw[0, 1], "x", ((1, 1),))
         b1_rows_f32 = keep.tile([P, P], F32)
         nc.vector.tensor_copy(out=b1_rows_f32[:], in_=b1_rows[:])
         b1_bank = psum.tile([P, P], F32, tag="y")
@@ -311,10 +327,6 @@ def tile_rssm_pa_kernel(
             nc.tensor.matmul(out=b2_bank[:], lhsT=ones[:], rhs=b2_row[:, cols], start=True, stop=True)
             nc.scalar.copy(out=b2_all[:, cols], in_=b2_bank[:])
 
-        weight_ready(0, 0)
-        weight_pass(0, 1)
-        x_ready(0, 0)
-        grouped_x[0, 1] = transpose_chunk(x_raw[0, 1], "x", ((1, 1),))
         weight_ready(0, 1)
         open_groups(LOW, "y", HALF)
         first_product(0, LOW, (0, 1), whole)
@@ -332,15 +344,6 @@ def tile_rssm_pa_kernel(
         weight_pass(0, 5)
         weight_ready(0, 5)
         first_product(0, LOW, (4, 5), whole)
-        x_raw[1, 1] = load_x(1, 1)
-        w_raw[1, 2] = load_w1(1, 2)
-        w_raw[1, 3] = load_w1(1, 3)
-        x_raw[1, 2] = load_x(1, 2)
-        w_raw[1, 4] = load_w1(1, 4)
-        w_raw[1, 5] = load_w1(1, 5)
-        w2_raw = [load_w2(0), load_w2(1)]
-        eps_all = keep.tile([P, HALVES, SUB, LATENT], BF16)
-        nc.sync.dma_start(out=eps_all[:], in_=eps.rearrange("(h p t) c -> p h t c", h=HALVES, t=SUB))
 
         hidden_low = leave_psum(LOW, (1,))
         x_ready(1, 0)
@@ -363,7 +366,7 @@ def tile_rssm_pa_kernel(
             weight_pass(1, g)
             first_product(0, HIGH, (g - 1,), whole)
             weight_ready(1, g)
-        grouped_h = group_hidden(hidden_low, HALF)
+        grouped_h = group_hidden(hidden_low, HALF, HALF)
         hidden_low = leave_psum(LOW, ())
         quantise_hidden(0, 0, HALF, grouped_h)
         for g in (4, 5):
@@ -374,29 +377,38 @@ def tile_rssm_pa_kernel(
         hidden_high = leave_psum(HIGH, (5, 7))
         for g in range(PASSES2):
             grouped_w[g] = group_w2(w2_raw[g])
-        grouped_l = group_hidden(hidden_low, HALF)
+        grouped_l = group_hidden(hidden_low, HALF, HALF)
         for g in range(PASSES2):
             for first, last in OUT_BANKS:
                 quantise_weight(w2_codes[:, g, :], w2_scales[:, g, :], grouped_w[g], slice(first, last))
-        grouped_h = group_hidden(hidden_high, HALF)
+        grouped_h = group_hidden(hidden_high, HALF, HALF)
         quantise_hidden(0, HALF, HALF, grouped_l)
         quantise_hidden(1, 0, HALF, grouped_h)
 
-        def last_tiles(quarter, bank_set):
-            hidden = hidden_pool.tile([P, PACK, QUARTER], BF16, name="hidden_q")
-            for h in HIGH:
+        def last_tiles(hidden, quarter, h_tiles, bank_set):
+            for h in h_tiles:
                 open_groups((h,), bank_set, QUARTER)
                 first_product(1, (h,), range(PASSES1), slice(quarter * QUARTER, (quarter + 1) * QUARTER))
                 relu_out(hidden, h, False)
-            return hidden
 
-        def last_hidden(quarter, hidden):
-            grouped = group_hidden(hidden, QUARTER)
+        def last_hidden(quarter, hidden, vector_cols):
+            grouped = group_hidden(hidden, QUARTER, vector_cols)
             quantise_hidden(1, HALF + quarter * QUARTER, QUARTER, grouped)
 
-        hidden_q = last_tiles(0, "y")
-        last_hidden(0, hidden_q)
-        finish_half(0, "x")
-        hidden_q = last_tiles(1, "y")
-        last_hidden(1, hidden_q)
-        finish_half(1, "x")
+        hidden_q = []
+        for quarter in range(2):
+            hidden_q.append(hidden_pool.tile([P, PACK, QUARTER], BF16, name="hidden_q"))
+        last_tiles(hidden_q[0], 0, HIGH[0:4], "y")
+        last_hidden(0, hidden_q[0], 0)
+        finish_tile(0, 0, "x")
+        finish_tile(0, 1, "x")
+        last_tiles(hidden_q[1], 1, HIGH[0:2], "y")
+        finish_tile(0, 2, "x")
+        finish_tile(0, 3, "x")
+        last_tiles(hidden_q[1], 1, HIGH[2:4], "y")
+        last_hidden(1, hidden_q[1], 128)
+        finish_tile(1, 0, "x")
+        finish_tile(1, 1, "x")
+        finish_tile(1, 2, "x")
+        finish_tile(1, 3, "x")
+        draw_sample(*waiting.pop())

@@ -10,7 +10,6 @@ U8 = mybir.dt.uint8
 FP8X4 = mybir.dt.float8_e4m3fn_x4
 ACT = mybir.ActivationFunctionType
 ALU = mybir.AluOpType
-PE = mybir.EngineType.PE
 
 P = 128
 PACK = 4
@@ -50,11 +49,11 @@ def tile_rssm_pa_kernel(
         x_raw_pool = ctx.enter_context(tc.tile_pool(name="x_raw", bufs=4))
         x_grp_pool = ctx.enter_context(tc.tile_pool(name="x_grp", bufs=4))
         w_raw_pool = ctx.enter_context(tc.tile_pool(name="w_raw", bufs=W_BUFS))
-        w_grp_pool = ctx.enter_context(tc.tile_pool(name="w_grp", bufs=3))
+        w_grp_pool = ctx.enter_context(tc.tile_pool(name="w_grp", bufs=4))
         hidden_pool = ctx.enter_context(tc.tile_pool(name="hidden", bufs=2))
-        result_pool = ctx.enter_context(tc.tile_pool(name="result", bufs=4))
+        result_pool = ctx.enter_context(tc.tile_pool(name="result", bufs=3))
         psum = ctx.enter_context(tc.psum_pool(name="psum", bufs=4))
-        ctx.enter_context(tc.manual_schedule(engines={PE}))
+        ctx.enter_context(tc.manual_schedule())
 
         def by_tile(dram):
             return dram.rearrange("(h p t) c -> h p t c", h=HALVES, t=SUB)
@@ -101,9 +100,9 @@ def tile_rssm_pa_kernel(
                 nc.sync.dma_start(out=raw[:, t, :], in_=rows[t])
             return raw
 
-        def transpose_chunk(raw, bank_set, vector_banks=()):
+        def transpose_chunk(raw, bank_set):
             words = raw[:].bitcast(F32)
-            banks = {}
+            banks = []
             for pair in range(SUB // 2):
                 for local in range(X_CHUNK // K_PASS):
                     bank = psum.tile([P, 2, 2 * P], F32, name="x_bank", tag=bank_set)
@@ -113,18 +112,18 @@ def tile_rssm_pa_kernel(
                             nc.tensor.transpose(
                                 out=bank[:, u, tt * P : (tt + 1) * P], in_=words[:, first + u : first + WORDS : 2], identity=ident[:]
                             )
-                    banks[local, pair] = bank
+                    banks.append(bank)
+            return banks
+
+        def copy_chunk(banks, vector_banks=()):
             grouped_tiles = []
             for local in range(X_CHUNK // K_PASS):
                 grouped_tiles.append(x_grp_pool.tile([P, HALF * PACK], BF16, name="x_grp", align_bytes=64))
-            for pair in range(SUB // 2):
-                for local in range(X_CHUNK // K_PASS):
-                    word_pairs = grouped_tiles[local][:].bitcast(F32).rearrange("p (c u) -> p c u", u=2)
-                    copy = nc.vector.tensor_copy if (pair, local) in vector_banks else nc.scalar.copy
-                    copy(
-                        out=word_pairs[:, pair * 2 * P : (pair + 1) * 2 * P, :],
-                        in_=banks[local, pair][:].rearrange("p u c -> p c u"),
-                    )
+            for n, bank in enumerate(banks):
+                pair, local = divmod(n, X_CHUNK // K_PASS)
+                word_pairs = grouped_tiles[local][:].bitcast(F32).rearrange("p (c u) -> p c u", u=2)
+                copy = nc.vector.tensor_copy if n in vector_banks else nc.scalar.copy
+                copy(out=word_pairs[:, pair * 2 * P : (pair + 1) * 2 * P, :], in_=bank[:].rearrange("p u c -> p c u"))
             return grouped_tiles
 
         def quantise_x(half, g, grouped):
@@ -140,7 +139,10 @@ def tile_rssm_pa_kernel(
             grouped = w_grp_pool.tile([P, K_PASS, PACK], BF16, name="w_grp", align_bytes=64)
             target = grouped[:].rearrange("p (t b i) j -> p t b j i", t=PACK, i=RUN)
             source = raw[:].rearrange("p j (b t i) -> p t b j i", t=PACK, i=RUN)
-            nc.vector.tensor_copy(out=target[:, 0:vector_tiles], in_=source[:, 0:vector_tiles])
+            if vector_tiles == 1:
+                nc.vector.tensor_copy(out=target[:, 0], in_=source[:, 0])
+            else:
+                nc.vector.tensor_copy(out=target[:, 0:vector_tiles], in_=source[:, 0:vector_tiles])
             for t in range(vector_tiles, PACK):
                 nc.scalar.copy(out=target[:, t], in_=source[:, t])
             return grouped
@@ -229,7 +231,8 @@ def tile_rssm_pa_kernel(
 
         def draw_sample(half, t, result, root):
             noise = result_pool.tile([P, LATENT], F32, name="noise")
-            nc.vector.tensor_tensor(out=noise[:], in0=root[:], in1=eps_all[:, half, t, :], op=ALU.mult)
+            product_engine = nc.gpsimd if half == 0 and t < 2 else nc.vector
+            product_engine.tensor_tensor(out=noise[:], in0=root[:], in1=eps_all[:, half, t, :], op=ALU.mult)
             sample = result_pool.tile([P, LATENT], F32, name="sample")
             sum_engine = nc.vector if half == 1 and t == SUB - 1 else nc.gpsimd
             sum_engine.tensor_tensor(out=sample[:], in0=noise[:], in1=result[:, 0:LATENT], op=ALU.add)
@@ -252,6 +255,10 @@ def tile_rssm_pa_kernel(
 
         x_raw = {}
         w_raw = {}
+        b1_runs = rep_b1.rearrange("(q b t i) -> q t b i", q=PASSES2, t=PACK, i=RUN)
+        for q in range(PASSES2):
+            nc.sync.dma_start(out=b1_rows[PACK * q : PACK * (q + 1), :].rearrange("t (b i) -> t b i", i=RUN), in_=b1_runs[q])
+        nc.sync.dma_start(out=b2_row[0:1, :], in_=rep_b2.rearrange("(o n) -> o n", o=1))
         x_raw[0, 0] = new_x()
         fill_x(x_raw[0, 0], 0, 0, slice(0, SUB // 2))
         fill_x(x_raw[0, 0], 0, 0, slice(SUB // 2, SUB))
@@ -259,19 +266,15 @@ def tile_rssm_pa_kernel(
         x_raw[0, 1] = load_x(0, 1)
         w_raw[0, 1] = load_w1(0, 1)
         w_raw[0, 2] = load_w1(0, 2)
-        b1_runs = rep_b1.rearrange("(q b t i) -> q t b i", q=PASSES2, t=PACK, i=RUN)
-        for q in range(PASSES2):
-            nc.sync.dma_start(out=b1_rows[PACK * q : PACK * (q + 1), :].rearrange("t (b i) -> t b i", i=RUN), in_=b1_runs[q])
-        nc.sync.dma_start(out=b2_row[0:1, :], in_=rep_b2.rearrange("(o n) -> o n", o=1))
         x_raw[0, 2] = load_x(0, 2)
         w_raw[0, 3] = load_w1(0, 3)
         w_raw[0, 4] = load_w1(0, 4)
         x_raw[1, 0] = load_x(1, 0)
         w_raw[0, 5] = load_w1(0, 5)
-        x_raw[1, 1] = load_x(1, 1)
-        x_raw[1, 2] = load_x(1, 2)
         w_raw[1, 0] = load_w1(1, 0)
+        x_raw[1, 1] = load_x(1, 1)
         w_raw[1, 1] = load_w1(1, 1)
+        x_raw[1, 2] = load_x(1, 2)
         w_raw[1, 2] = load_w1(1, 2)
         w_raw[1, 3] = load_w1(1, 3)
         w_raw[1, 4] = load_w1(1, 4)
@@ -308,12 +311,13 @@ def tile_rssm_pa_kernel(
                 in_=grouped_w[q, g][:].rearrange("p w t -> p (w t)"),
             )
 
-        weight_pass(0, 0)
-        grouped_x[0, 0] = transpose_chunk(x_raw[0, 0], "x", ((0, 1), (1, 1)))
-        weight_ready(0, 0)
-        weight_pass(0, 1)
-        x_ready(0, 0)
-        grouped_x[0, 1] = transpose_chunk(x_raw[0, 1], "x", ((1, 1),))
+        def copies(half, chunk, vector_banks=()):
+            grouped_x[half, chunk] = copy_chunk(x_banks[half, chunk], vector_banks)
+
+        def turn(half, chunk):
+            x_banks[half, chunk] = transpose_chunk(x_raw[half, chunk], "x")
+
+        x_banks = {}
         b1_rows_f32 = keep.tile([P, P], F32)
         nc.vector.tensor_copy(out=b1_rows_f32[:], in_=b1_rows[:])
         b1_bank = psum.tile([P, P], F32, tag="y")
@@ -327,63 +331,75 @@ def tile_rssm_pa_kernel(
             nc.tensor.matmul(out=b2_bank[:], lhsT=ones[:], rhs=b2_row[:, cols], start=True, stop=True)
             nc.scalar.copy(out=b2_all[:, cols], in_=b2_bank[:])
 
+        turn(0, 0)
+        copies(0, 0, (1, 3))
+        weight_pass(0, 0, 2)
+        x_ready(0, 0)
+        weight_ready(0, 0)
+        weight_pass(0, 1, 2)
+        turn(0, 1)
+        copies(0, 1, (3,))
         weight_ready(0, 1)
+        weight_pass(0, 2, 2)
+
         open_groups(LOW, "y", HALF)
         first_product(0, LOW, (0, 1), whole)
-        weight_pass(0, 2)
         x_ready(0, 1)
-        grouped_x[0, 2] = transpose_chunk(x_raw[0, 2], "x", ((1, 1),))
         weight_ready(0, 2)
-        weight_pass(0, 3)
+        weight_pass(0, 3, 2)
+        turn(0, 2)
+        copies(0, 2, (3,))
         weight_ready(0, 3)
+        weight_pass(0, 4, 2)
         first_product(0, LOW, (2, 3), whole)
-        weight_pass(0, 4)
         x_ready(0, 2)
         weight_ready(0, 4)
-        grouped_x[1, 0] = transpose_chunk(x_raw[1, 0], "x", ((1, 1),))
-        weight_pass(0, 5)
+        weight_pass(0, 5, 2)
+        turn(1, 0)
+        copies(1, 0, (3,))
         weight_ready(0, 5)
         first_product(0, LOW, (4, 5), whole)
-
-        hidden_low = leave_psum(LOW, (1,))
+        weight_pass(1, 0, 2)
         x_ready(1, 0)
-        grouped_x[1, 1] = transpose_chunk(x_raw[1, 1], "x", ((1, 1),))
+        weight_ready(1, 0)
+        turn(1, 1)
+        hidden_low = leave_psum(LOW, (1,))
+        copies(1, 1, (3,))
+        weight_pass(1, 1, 2)
         open_groups(LOW, "y", HALF)
         first_product(1, LOW, (0, 1), whole)
         x_ready(1, 1)
-        weight_pass(1, 0)
-        weight_ready(1, 0)
-        grouped_x[1, 2] = transpose_chunk(x_raw[1, 2], "x", ((1, 1),))
-        first_product(1, LOW, (2, 3), whole)
-        weight_pass(1, 1)
-        x_ready(1, 2)
         weight_ready(1, 1)
+        turn(1, 2)
+        copies(1, 2, (3,))
+        weight_pass(1, 2, 2)
+        first_product(1, LOW, (2, 3), whole)
+        x_ready(1, 2)
+        weight_ready(1, 2)
+        weight_pass(1, 3, 2)
+        weight_ready(1, 3)
 
         open_groups(HIGH, "x", HALF)
         first_product(0, HIGH, (0,), whole)
         first_product(1, LOW, (4, 5), whole)
-        for g in (2, 3):
-            weight_pass(1, g)
-            first_product(0, HIGH, (g - 1,), whole)
-            weight_ready(1, g)
+        weight_pass(1, 4, 2)
         grouped_h = group_hidden(hidden_low, HALF, HALF)
-        hidden_low = leave_psum(LOW, ())
+        weight_ready(1, 4)
+        weight_pass(1, 5, 2)
         quantise_hidden(0, 0, HALF, grouped_h)
-        for g in (4, 5):
-            weight_pass(1, g)
-            first_product(0, HIGH, (g - 1,), whole)
-            weight_ready(1, g)
-        first_product(0, HIGH, (5,), whole)
-        hidden_high = leave_psum(HIGH, (5, 7))
+        weight_ready(1, 5)
+        first_product(0, HIGH, (1, 2, 3, 4, 5), whole)
+        hidden_low = leave_psum(LOW, ())
         for g in range(PASSES2):
             grouped_w[g] = group_w2(w2_raw[g])
-        grouped_l = group_hidden(hidden_low, HALF, HALF)
         for g in range(PASSES2):
             for first, last in OUT_BANKS:
                 quantise_weight(w2_codes[:, g, :], w2_scales[:, g, :], grouped_w[g], slice(first, last))
+        hidden_high = leave_psum(HIGH, (5,))
         grouped_h = group_hidden(hidden_high, HALF, HALF)
-        quantise_hidden(0, HALF, HALF, grouped_l)
+        grouped_l = group_hidden(hidden_low, HALF, HALF)
         quantise_hidden(1, 0, HALF, grouped_h)
+        quantise_hidden(0, HALF, HALF, grouped_l)
 
         def last_tiles(hidden, quarter, h_tiles, bank_set):
             for h in h_tiles:
@@ -400,13 +416,13 @@ def tile_rssm_pa_kernel(
             hidden_q.append(hidden_pool.tile([P, PACK, QUARTER], BF16, name="hidden_q"))
         last_tiles(hidden_q[0], 0, HIGH[0:4], "y")
         last_hidden(0, hidden_q[0], 0)
+        last_tiles(hidden_q[1], 1, HIGH[0:2], "y")
         finish_tile(0, 0, "x")
         finish_tile(0, 1, "x")
-        last_tiles(hidden_q[1], 1, HIGH[0:2], "y")
-        finish_tile(0, 2, "x")
-        finish_tile(0, 3, "x")
         last_tiles(hidden_q[1], 1, HIGH[2:4], "y")
         last_hidden(1, hidden_q[1], 128)
+        finish_tile(0, 2, "x")
+        finish_tile(0, 3, "x")
         finish_tile(1, 0, "x")
         finish_tile(1, 1, "x")
         finish_tile(1, 2, "x")

@@ -233,7 +233,7 @@ def tile_rssm_pa_kernel(
             noise = result_pool.tile([P, LATENT], F32, name="noise")
             product_engine = nc.gpsimd if half == 0 and t < 2 else nc.vector
             product_engine.tensor_tensor(out=noise[:], in0=root[:], in1=eps_all[:, half, t, :], op=ALU.mult)
-            sample = result_pool.tile([P, LATENT], F32, name="sample")
+            sample = result_pool.tile([P, LATENT], F32, name="sample", bufs=SUB)
             sum_engine = nc.vector if half == 1 and t == SUB - 1 else nc.gpsimd
             sum_engine.tensor_tensor(out=sample[:], in0=noise[:], in1=result[:, 0:LATENT], op=ALU.add)
             nc.sync.dma_start(out=outputs[2][half, :, t, :], in_=sample[:])
@@ -246,7 +246,7 @@ def tile_rssm_pa_kernel(
                 draw_sample(*waiting.pop())
             waiting.append((half, t, result, root))
 
-        ones = keep.tile([P, P], BF16)
+        ones = keep.tile([P, HALF], BF16)
         nc.vector.memset(ones[:], 1.0)
         b1_rows = keep.tile([P, P], BF16)
         nc.vector.memset(b1_rows[:], 0.0)
@@ -255,14 +255,14 @@ def tile_rssm_pa_kernel(
 
         x_raw = {}
         w_raw = {}
-        b1_runs = rep_b1.rearrange("(q b t i) -> q t b i", q=PASSES2, t=PACK, i=RUN)
-        for q in range(PASSES2):
-            nc.sync.dma_start(out=b1_rows[PACK * q : PACK * (q + 1), :].rearrange("t (b i) -> t b i", i=RUN), in_=b1_runs[q])
-        nc.sync.dma_start(out=b2_row[0:1, :], in_=rep_b2.rearrange("(o n) -> o n", o=1))
         x_raw[0, 0] = new_x()
         fill_x(x_raw[0, 0], 0, 0, slice(0, SUB // 2))
         fill_x(x_raw[0, 0], 0, 0, slice(SUB // 2, SUB))
         w_raw[0, 0] = load_w1(0, 0)
+        b1_runs = rep_b1.rearrange("(q b t i) -> q t b i", q=PASSES2, t=PACK, i=RUN)
+        for q in range(PASSES2):
+            nc.sync.dma_start(out=b1_rows[PACK * q : PACK * (q + 1), :].rearrange("t (b i) -> t b i", i=RUN), in_=b1_runs[q])
+        nc.sync.dma_start(out=b2_row[0:1, :], in_=rep_b2.rearrange("(o n) -> o n", o=1))
         x_raw[0, 1] = load_x(0, 1)
         w_raw[0, 1] = load_w1(0, 1)
         w_raw[0, 2] = load_w1(0, 2)
@@ -317,7 +317,20 @@ def tile_rssm_pa_kernel(
         def turn(half, chunk):
             x_banks[half, chunk] = transpose_chunk(x_raw[half, chunk], "x")
 
+        def keep_busy(count):
+            idle = psum.tile([P, HALF], F32, name="idle", tag="y")
+            for n in range(count):
+                nc.tensor.matmul(out=idle[:], lhsT=ones[:, 0:P], rhs=ones[:], start=True, stop=True)
+
+        def quantise_w2(g):
+            for first, last in OUT_BANKS:
+                quantise_weight(w2_codes[:, g, :], w2_scales[:, g, :], grouped_w[g], slice(first, last))
+
         x_banks = {}
+        keep_busy(6)
+        turn(0, 0)
+        copies(0, 0, (1, 3))
+        weight_pass(0, 0, 2)
         b1_rows_f32 = keep.tile([P, P], F32)
         nc.vector.tensor_copy(out=b1_rows_f32[:], in_=b1_rows[:])
         b1_bank = psum.tile([P, P], F32, tag="y")
@@ -328,15 +341,13 @@ def tile_rssm_pa_kernel(
         for first, last in OUT_BANKS:
             cols = slice(first, last)
             b2_bank = psum.tile([P, last - first], F32, name="b2_bank", tag="y")
-            nc.tensor.matmul(out=b2_bank[:], lhsT=ones[:], rhs=b2_row[:, cols], start=True, stop=True)
+            nc.tensor.matmul(out=b2_bank[:], lhsT=ones[:, 0:P], rhs=b2_row[:, cols], start=True, stop=True)
             nc.scalar.copy(out=b2_all[:, cols], in_=b2_bank[:])
 
-        turn(0, 0)
-        copies(0, 0, (1, 3))
-        weight_pass(0, 0, 2)
         x_ready(0, 0)
         weight_ready(0, 0)
         weight_pass(0, 1, 2)
+        keep_busy(4)
         turn(0, 1)
         copies(0, 1, (3,))
         weight_ready(0, 1)
@@ -392,14 +403,11 @@ def tile_rssm_pa_kernel(
         hidden_low = leave_psum(LOW, ())
         for g in range(PASSES2):
             grouped_w[g] = group_w2(w2_raw[g])
-        for g in range(PASSES2):
-            for first, last in OUT_BANKS:
-                quantise_weight(w2_codes[:, g, :], w2_scales[:, g, :], grouped_w[g], slice(first, last))
+        quantise_w2(0)
         hidden_high = leave_psum(HIGH, (5,))
-        grouped_h = group_hidden(hidden_high, HALF, HALF)
-        grouped_l = group_hidden(hidden_low, HALF, HALF)
+        grouped_h = group_hidden(hidden_high, HALF, 384)
+        quantise_w2(1)
         quantise_hidden(1, 0, HALF, grouped_h)
-        quantise_hidden(0, HALF, HALF, grouped_l)
 
         def last_tiles(hidden, quarter, h_tiles, bank_set):
             for h in h_tiles:
@@ -415,14 +423,16 @@ def tile_rssm_pa_kernel(
         for quarter in range(2):
             hidden_q.append(hidden_pool.tile([P, PACK, QUARTER], BF16, name="hidden_q"))
         last_tiles(hidden_q[0], 0, HIGH[0:4], "y")
+        grouped_l = group_hidden(hidden_low, HALF, HALF)
         last_hidden(0, hidden_q[0], 0)
         last_tiles(hidden_q[1], 1, HIGH[0:2], "y")
         finish_tile(0, 0, "x")
+        quantise_hidden(0, HALF, HALF, grouped_l)
         finish_tile(0, 1, "x")
         last_tiles(hidden_q[1], 1, HIGH[2:4], "y")
-        last_hidden(1, hidden_q[1], 128)
         finish_tile(0, 2, "x")
         finish_tile(0, 3, "x")
+        last_hidden(1, hidden_q[1], 128)
         finish_tile(1, 0, "x")
         finish_tile(1, 1, "x")
         finish_tile(1, 2, "x")

@@ -100,31 +100,27 @@ def tile_rssm_pa_kernel(
                 nc.sync.dma_start(out=raw[:, t, :], in_=rows[t])
             return raw
 
-        def transpose_chunk(raw, bank_set):
+        def transpose_pair(raw, pair, bank_set):
             words = raw[:].bitcast(F32)
             banks = []
-            for pair in range(SUB // 2):
-                for local in range(X_CHUNK // K_PASS):
-                    bank = psum.tile([P, 2, 2 * P], F32, name="x_bank", tag=bank_set)
-                    for tt in range(2):
-                        for u in range(2):
-                            first = (2 * pair + tt) * (X_CHUNK // 2) + local * WORDS
-                            nc.tensor.transpose(
-                                out=bank[:, u, tt * P : (tt + 1) * P], in_=words[:, first + u : first + WORDS : 2], identity=ident[:]
-                            )
-                    banks.append(bank)
+            for local in range(X_CHUNK // K_PASS):
+                bank = psum.tile([P, 2, 2 * P], F32, name="x_bank", tag=bank_set)
+                for tt in range(2):
+                    for u in range(2):
+                        first = (2 * pair + tt) * (X_CHUNK // 2) + local * WORDS
+                        nc.tensor.transpose(
+                            out=bank[:, u, tt * P : (tt + 1) * P], in_=words[:, first + u : first + WORDS : 2], identity=ident[:]
+                        )
+                banks.append(bank)
             return banks
 
-        def copy_chunk(banks, vector_banks=()):
-            grouped_tiles = []
-            for local in range(X_CHUNK // K_PASS):
-                grouped_tiles.append(x_grp_pool.tile([P, HALF * PACK], BF16, name="x_grp", align_bytes=64))
-            for n, bank in enumerate(banks):
-                pair, local = divmod(n, X_CHUNK // K_PASS)
-                word_pairs = grouped_tiles[local][:].bitcast(F32).rearrange("p (c u) -> p c u", u=2)
-                copy = nc.vector.tensor_copy if n in vector_banks else nc.scalar.copy
+        def new_grouped():
+            return [x_grp_pool.tile([P, HALF * PACK], BF16, name="x_grp", align_bytes=64) for local in range(X_CHUNK // K_PASS)]
+
+        def copy_pair(grouped_tiles, banks, pair, engines):
+            for grouped, bank, copy in zip(grouped_tiles, banks, engines):
+                word_pairs = grouped[:].bitcast(F32).rearrange("p (c u) -> p c u", u=2)
                 copy(out=word_pairs[:, pair * 2 * P : (pair + 1) * 2 * P, :], in_=bank[:].rearrange("p u c -> p c u"))
-            return grouped_tiles
 
         def quantise_x(half, g, grouped):
             nc.vector.quantize_mx(out=x_codes[:, half, g, :].bitcast(FP8X4), scales=x_scales[:, half, g, :], in_=grouped[:])
@@ -311,11 +307,11 @@ def tile_rssm_pa_kernel(
                 in_=grouped_w[q, g][:].rearrange("p w t -> p (w t)"),
             )
 
-        def copies(half, chunk, vector_banks=()):
-            grouped_x[half, chunk] = copy_chunk(x_banks[half, chunk], vector_banks)
-
-        def turn(half, chunk):
-            x_banks[half, chunk] = transpose_chunk(x_raw[half, chunk], "x")
+        def turn(half, chunk, pair, engines):
+            if pair == 0:
+                grouped_x[half, chunk] = new_grouped()
+            banks = transpose_pair(x_raw[half, chunk], pair, "x")
+            copy_pair(grouped_x[half, chunk], banks, pair, engines)
 
         def keep_busy(count):
             idle = psum.tile([P, HALF], F32, name="idle", tag="y")
@@ -326,65 +322,66 @@ def tile_rssm_pa_kernel(
             for first, last in OUT_BANKS:
                 quantise_weight(w2_codes[:, g, :], w2_scales[:, g, :], grouped_w[g], slice(first, last))
 
-        x_banks = {}
+        scalar_both = (nc.scalar.copy, nc.scalar.copy)
+        shared = (nc.scalar.copy, nc.vector.tensor_copy)
+
         keep_busy(6)
-        turn(0, 0)
-        copies(0, 0, (1, 3))
+        turn(0, 0, 0, shared)
+        turn(0, 0, 1, shared)
         weight_pass(0, 0, 2)
+        keep_busy(6)
         b1_rows_f32 = keep.tile([P, P], F32)
         nc.vector.tensor_copy(out=b1_rows_f32[:], in_=b1_rows[:])
-        b1_bank = psum.tile([P, P], F32, tag="y")
+        b1_bank = psum.tile([P, P], F32, name="b1_bank", tag="y")
         nc.tensor.transpose(out=b1_bank[:], in_=b1_rows_f32[:], identity=ident[:])
+        b2_banks = []
+        for first, last in OUT_BANKS:
+            b2_banks.append(psum.tile([P, last - first], F32, name="b2_bank", tag="y"))
+            nc.tensor.matmul(out=b2_banks[-1][:], lhsT=ones[:, 0:P], rhs=b2_row[:, first:last], start=True, stop=True)
         b1_col = keep.tile([P, H_TILES], F32)
         nc.vector.tensor_copy(out=b1_col[:], in_=b1_bank[:, 0:H_TILES])
         b2_all = keep.tile([P, OUT], F32)
-        for first, last in OUT_BANKS:
-            cols = slice(first, last)
-            b2_bank = psum.tile([P, last - first], F32, name="b2_bank", tag="y")
-            nc.tensor.matmul(out=b2_bank[:], lhsT=ones[:, 0:P], rhs=b2_row[:, cols], start=True, stop=True)
-            nc.scalar.copy(out=b2_all[:, cols], in_=b2_bank[:])
-
+        for bank, (first, last) in zip(b2_banks, OUT_BANKS):
+            nc.scalar.copy(out=b2_all[:, first:last], in_=bank[:])
         x_ready(0, 0)
         weight_ready(0, 0)
         weight_pass(0, 1, 2)
-        keep_busy(4)
-        turn(0, 1)
-        copies(0, 1, (3,))
+        turn(0, 1, 0, scalar_both)
+        turn(0, 1, 1, shared)
         weight_ready(0, 1)
         weight_pass(0, 2, 2)
-
         open_groups(LOW, "y", HALF)
-        first_product(0, LOW, (0, 1), whole)
+        first_product(0, LOW, (0, 1,), whole)
         x_ready(0, 1)
         weight_ready(0, 2)
         weight_pass(0, 3, 2)
-        turn(0, 2)
-        copies(0, 2, (3,))
+        turn(0, 2, 0, scalar_both)
+        turn(0, 2, 1, shared)
         weight_ready(0, 3)
         weight_pass(0, 4, 2)
-        first_product(0, LOW, (2, 3), whole)
+        first_product(0, LOW, (2, 3,), whole)
         x_ready(0, 2)
         weight_ready(0, 4)
         weight_pass(0, 5, 2)
-        turn(1, 0)
-        copies(1, 0, (3,))
+        turn(1, 0, 0, scalar_both)
+        turn(1, 0, 1, shared)
         weight_ready(0, 5)
-        first_product(0, LOW, (4, 5), whole)
+        first_product(0, LOW, (4, 5,), whole)
         weight_pass(1, 0, 2)
         x_ready(1, 0)
         weight_ready(1, 0)
-        turn(1, 1)
         hidden_low = leave_psum(LOW, (1,))
-        copies(1, 1, (3,))
+        turn(1, 1, 0, scalar_both)
+        turn(1, 1, 1, shared)
         weight_pass(1, 1, 2)
         open_groups(LOW, "y", HALF)
-        first_product(1, LOW, (0, 1), whole)
+        first_product(1, LOW, (0, 1,), whole)
         x_ready(1, 1)
         weight_ready(1, 1)
-        turn(1, 2)
-        copies(1, 2, (3,))
+        turn(1, 2, 0, scalar_both)
+        turn(1, 2, 1, shared)
         weight_pass(1, 2, 2)
-        first_product(1, LOW, (2, 3), whole)
+        first_product(1, LOW, (2, 3,), whole)
         x_ready(1, 2)
         weight_ready(1, 2)
         weight_pass(1, 3, 2)

@@ -61,14 +61,14 @@ def tile_rssm_pa_kernel(
         x_sources = ((by_tile(prev_state), 0), (by_tile(prev_action), STATE), (by_tile(observation), STATE + ACTION))
         outputs = (by_tile(out_0), by_tile(out_1), by_tile(out_2))
 
-        x_codes = keep.tile([P, HALVES, PASSES1, HALF], U32, align_bytes=64)
-        x_scales = keep.tile([P, HALVES, PASSES1, HALF], U8, align_bytes=64)
-        w1_codes = keep.tile([P, PASSES1, HIDDEN], U32, align_bytes=64)
-        w1_scales = keep.tile([P, PASSES1, HIDDEN], U8, align_bytes=64)
-        h1_codes = keep.tile([P, PASSES2, BATCH], U32, align_bytes=64)
-        h1_scales = keep.tile([P, PASSES2, BATCH], U8, align_bytes=64)
-        w2_codes = keep.tile([P, PASSES2, OUT], U32, align_bytes=64)
-        w2_scales = keep.tile([P, PASSES2, OUT], U8, align_bytes=64)
+        x_codes = keep.tile([P, HALVES, PASSES1, HALF], U32, align_bytes=256)
+        x_scales = keep.tile([P, HALVES, PASSES1, HALF], U8, align_bytes=256)
+        w1_codes = keep.tile([P, PASSES1, HIDDEN], U32, align_bytes=256)
+        w1_scales = keep.tile([P, PASSES1, HIDDEN], U8, align_bytes=256)
+        h1_codes = keep.tile([P, PASSES2, BATCH], U32, align_bytes=256)
+        h1_scales = keep.tile([P, PASSES2, BATCH], U8, align_bytes=256)
+        w2_codes = keep.tile([P, PASSES2, OUT], U32, align_bytes=256)
+        w2_scales = keep.tile([P, PASSES2, OUT], U8, align_bytes=256)
 
         def new_x():
             return x_raw_pool.tile([P, SUB * X_CHUNK], BF16, name="x_raw")
@@ -246,8 +246,6 @@ def tile_rssm_pa_kernel(
         nc.vector.memset(ones[:], 1.0)
         b1_rows = keep.tile([P, P], BF16)
         nc.vector.memset(b1_rows[:], 0.0)
-        b2_row = keep.tile([P, OUT], BF16)
-        nc.vector.memset(b2_row[:], 0.0)
 
         x_raw = {}
         w_raw = {}
@@ -258,7 +256,6 @@ def tile_rssm_pa_kernel(
         b1_runs = rep_b1.rearrange("(q b t i) -> q t b i", q=PASSES2, t=PACK, i=RUN)
         for q in range(PASSES2):
             nc.sync.dma_start(out=b1_rows[PACK * q : PACK * (q + 1), :].rearrange("t (b i) -> t b i", i=RUN), in_=b1_runs[q])
-        nc.sync.dma_start(out=b2_row[0:1, :], in_=rep_b2.rearrange("(o n) -> o n", o=1))
         x_raw[0, 1] = load_x(0, 1)
         w_raw[0, 1] = load_w1(0, 1)
         w_raw[0, 2] = load_w1(0, 2)
@@ -276,6 +273,8 @@ def tile_rssm_pa_kernel(
         w_raw[1, 4] = load_w1(1, 4)
         w_raw[1, 5] = load_w1(1, 5)
         w2_raw = [load_w2(0), load_w2(1)]
+        b2_all = keep.tile([P, OUT], BF16)
+        nc.sync.dma_start(out=b2_all[:], in_=rep_b2.partition_broadcast(P))
         eps_all = keep.tile([P, HALVES, SUB, LATENT], BF16)
         nc.sync.dma_start(out=eps_all[:], in_=eps.rearrange("(h p t) c -> p h t c", h=HALVES, t=SUB))
 
@@ -334,15 +333,8 @@ def tile_rssm_pa_kernel(
         nc.vector.tensor_copy(out=b1_rows_f32[:], in_=b1_rows[:])
         b1_bank = psum.tile([P, P], F32, name="b1_bank", tag="y")
         nc.tensor.transpose(out=b1_bank[:], in_=b1_rows_f32[:], identity=ident[:])
-        b2_banks = []
-        for first, last in OUT_BANKS:
-            b2_banks.append(psum.tile([P, last - first], F32, name="b2_bank", tag="y"))
-            nc.tensor.matmul(out=b2_banks[-1][:], lhsT=ones[:, 0:P], rhs=b2_row[:, first:last], start=True, stop=True)
         b1_col = keep.tile([P, H_TILES], F32)
         nc.vector.tensor_copy(out=b1_col[:], in_=b1_bank[:, 0:H_TILES])
-        b2_all = keep.tile([P, OUT], F32)
-        for bank, (first, last) in zip(b2_banks, OUT_BANKS):
-            nc.scalar.copy(out=b2_all[:, first:last], in_=bank[:])
         x_ready(0, 0)
         weight_ready(0, 0)
         weight_pass(0, 1, 2)

@@ -127,8 +127,8 @@ def tile_rssm_pa_kernel(
 
         def group_rows(copy, grouped, raw, cols):
             copy(
-                out=grouped[:, cols, :].rearrange("p (c i) t -> p c t i", i=4),
-                in_=raw[:, :, cols].rearrange("p t (c i) -> p c t i", i=4),
+                out=grouped[:, cols, :].rearrange("p (c i) t -> p c t i", i=RUN),
+                in_=raw[:, :, cols].rearrange("p t (c i) -> p c t i", i=RUN),
             )
 
         def group_w1(raw, vector_tiles):

from contextlib import ExitStack

import concourse.mybir as mybir
from concourse.masks import make_identity

F32 = mybir.dt.float32
BF16 = mybir.dt.bfloat16
U32 = mybir.dt.uint32
U8 = mybir.dt.uint8
FP8X4 = mybir.dt.float8_e4m3fn_x4
ACT = mybir.ActivationFunctionType
ALU = mybir.AluOpType

P = 128
PACK = 4
K_PASS = P * PACK

BATCH, STATE, ACTION, OBS, HIDDEN, LATENT = 1024, 1024, 128, 1920, 1024, 384
K1 = STATE + ACTION + OBS
OUT = 2 * LATENT
PASSES1 = K1 // K_PASS
PASSES2 = HIDDEN // K_PASS

HALF = 512
HALVES = BATCH // HALF
QUARTER = HALF // 2
SUB = HALF // P
X_CHUNK = 2 * K_PASS
CHUNKS = K1 // X_CHUNK
WORDS = K_PASS // 2

W_BUFS = 6
RUN = 8
H_TILES = HIDDEN // P
LOW = (0, 1, 2, 3)
HIGH = (4, 5, 6, 7)

OUT_BANKS = ((OUT - HALF, OUT), (0, OUT - HALF))

FLOPS = 2 * BATCH * K1 * HIDDEN + 2 * BATCH * HIDDEN * OUT


def tile_rssm_pa_kernel(
    tc, prev_state, prev_action, observation, eps, rep_W1, rep_b1, rep_W2, rep_b2, out_0, out_1, out_2
):
    nc = tc.nc
    with ExitStack() as ctx:
        keep = ctx.enter_context(tc.tile_pool(name="keep", bufs=1))
        x_raw_pool = ctx.enter_context(tc.tile_pool(name="x_raw", bufs=4))
        x_grp_pool = ctx.enter_context(tc.tile_pool(name="x_grp", bufs=4))
        w_raw_pool = ctx.enter_context(tc.tile_pool(name="w_raw", bufs=W_BUFS))
        w_grp_pool = ctx.enter_context(tc.tile_pool(name="w_grp", bufs=4))
        hidden_pool = ctx.enter_context(tc.tile_pool(name="hidden", bufs=2))
        result_pool = ctx.enter_context(tc.tile_pool(name="result", bufs=3))
        psum = ctx.enter_context(tc.psum_pool(name="psum", bufs=4))
        ctx.enter_context(tc.manual_schedule())

        def by_tile(dram):
            return dram.rearrange("(h p t) c -> h p t c", h=HALVES, t=SUB)

        x_sources = ((by_tile(prev_state), 0), (by_tile(prev_action), STATE), (by_tile(observation), STATE + ACTION))
        outputs = (by_tile(out_0), by_tile(out_1), by_tile(out_2))

        x_codes = keep.tile([P, HALVES, PASSES1, HALF], U32, align_bytes=256)
        x_scales = keep.tile([P, HALVES, PASSES1, HALF], U8, align_bytes=256)
        w1_codes = keep.tile([P, PASSES1, HIDDEN], U32, align_bytes=256)
        w1_scales = keep.tile([P, PASSES1, HIDDEN], U8, align_bytes=256)
        h1_codes = keep.tile([P, PASSES2, BATCH], U32, align_bytes=256)
        h1_scales = keep.tile([P, PASSES2, BATCH], U8, align_bytes=256)
        w2_codes = keep.tile([P, PASSES2, OUT], U32, align_bytes=256)
        w2_scales = keep.tile([P, PASSES2, OUT], U8, align_bytes=256)

        def new_x():
            return x_raw_pool.tile([P, SUB * X_CHUNK], BF16, name="x_raw")

        def fill_x(raw, half, chunk, tiles):
            rows = raw[:].rearrange("p (t k) -> p t k", t=SUB)
            first = chunk * X_CHUNK
            for source, start in x_sources:
                lo = max(start, first)
                hi = min(start + source.shape[3], first + X_CHUNK)
                if lo < hi:
                    nc.sync.dma_start(out=rows[:, tiles, lo - first : hi - first], in_=source[half, :, tiles, lo - start : hi - start])

        def load_x(half, chunk):
            raw = new_x()
            fill_x(raw, half, chunk, slice(0, SUB))
            return raw

        def load_w1(q, g):
            raw = w_raw_pool.tile([P, PACK, K_PASS], BF16, name="w1_raw", tag="w_raw", bufs=W_BUFS)
            rows = rep_W1[g * K_PASS : (g + 1) * K_PASS, q * K_PASS : (q + 1) * K_PASS]
            nc.sync.dma_start(out=raw[:], in_=rows.rearrange("(p j) w -> p j w", j=PACK))
            return raw

        def load_w2(g):
            raw = w_raw_pool.tile([P, PACK, OUT], BF16, name="w2_raw", tag="w2_raw", bufs=PASSES2)
            rows = rep_W2[g * K_PASS : (g + 1) * K_PASS, :].rearrange("(b t i) n -> t b i n", t=PACK, i=RUN)
            for t in range(PACK):
                nc.sync.dma_start(out=raw[:, t, :], in_=rows[t])
            return raw

        def transpose_pair(raw, pair, bank_set):
            words = raw[:].bitcast(F32)
            banks = []
            for local in range(X_CHUNK // K_PASS):
                bank = psum.tile([P, 2, 2 * P], F32, name="x_bank", tag=bank_set)
                for tt in range(2):
                    for u in range(2):
                        first = (2 * pair + tt) * (X_CHUNK // 2) + local * WORDS
                        nc.tensor.transpose(
                            out=bank[:, u, tt * P : (tt + 1) * P], in_=words[:, first + u : first + WORDS : 2], identity=ident[:]
                        )
                banks.append(bank)
            return banks

        def new_grouped():
            return [x_grp_pool.tile([P, HALF * PACK], BF16, name="x_grp", align_bytes=64) for local in range(X_CHUNK // K_PASS)]

        def copy_pair(grouped_tiles, banks, pair, engines):
            for grouped, bank, copy in zip(grouped_tiles, banks, engines):
                word_pairs = grouped[:].bitcast(F32).rearrange("p (c u) -> p c u", u=2)
                copy(out=word_pairs[:, pair * 2 * P : (pair + 1) * 2 * P, :], in_=bank[:].rearrange("p u c -> p c u"))

        def quantise_x(half, g, grouped):
            nc.vector.quantize_mx(out=x_codes[:, half, g, :].bitcast(FP8X4), scales=x_scales[:, half, g, :], in_=grouped[:])

        def group_rows(copy, grouped, raw, cols):
            copy(
                out=grouped[:, cols, :].rearrange("p (c i) t -> p c t i", i=RUN),
                in_=raw[:, :, cols].rearrange("p t (c i) -> p c t i", i=RUN),
            )

        def group_w1(raw, vector_tiles):
            grouped = w_grp_pool.tile([P, K_PASS, PACK], BF16, name="w_grp", align_bytes=64)
            target = grouped[:].rearrange("p (t b i) j -> p t b j i", t=PACK, i=RUN)
            source = raw[:].rearrange("p j (b t i) -> p t b j i", t=PACK, i=RUN)
            if vector_tiles == 1:
                nc.vector.tensor_copy(out=target[:, 0], in_=source[:, 0])
            else:
                nc.vector.tensor_copy(out=target[:, 0:vector_tiles], in_=source[:, 0:vector_tiles])
            for t in range(vector_tiles, PACK):
                nc.scalar.copy(out=target[:, t], in_=source[:, t])
            return grouped

        def group_w2(raw):
            grouped = w_grp_pool.tile([P, OUT, PACK], BF16, name="w2_grp", align_bytes=64, bufs=2)
            group_rows(nc.vector.tensor_copy, grouped, raw, slice(0, OUT // 2))
            group_rows(nc.scalar.copy, grouped, raw, slice(OUT // 2, OUT))
            return grouped

        def quantise_weight(codes, scales, grouped, cols):
            nc.vector.quantize_mx(
                out=codes[:, cols].bitcast(FP8X4),
                scales=scales[:, cols],
                in_=grouped[:, cols, :].rearrange("p w t -> p (w t)"),
            )

        def open_groups(h_tiles, bank_set, width):
            for h in h_tiles:
                acc[h] = psum.tile([P, width], F32, name="acc", tag=bank_set)

        def first_product(half, h_tiles, passes, cols):
            for g in passes:
                for h in h_tiles:
                    first = h * P
                    nc.tensor.matmul_mx(
                        out=acc[h][:],
                        lhsT=w1_codes[:, g, first : first + P].bitcast(FP8X4),
                        lhsT_scale=w1_scales[:, g, first : first + P],
                        rhs=x_codes[:, half, g, cols].bitcast(FP8X4),
                        rhs_scale=x_scales[:, half, g, cols],
                        start=(g == 0),
                        stop=(g == PASSES1 - 1),
                    )

        def relu_out(hidden, h, on_vector):
            if on_vector:
                nc.vector.tensor_scalar(
                    out=hidden[:, h % PACK, :], in0=acc[h][:], scalar1=b1_col[:, h : h + 1], scalar2=0.0, op0=ALU.add, op1=ALU.max
                )
            else:
                nc.scalar.activation(out=hidden[:, h % PACK, :], in_=acc[h][:], func=ACT.Relu, bias=b1_col[:, h : h + 1], scale=1.0)

        def leave_psum(h_tiles, vector_tiles):
            hidden = hidden_pool.tile([P, PACK, HALF], BF16, name="hidden")
            for h in h_tiles:
                relu_out(hidden, h, h in vector_tiles)
            return hidden

        def group_hidden(hidden, width, vector_cols):
            grouped = hidden_pool.tile([P, width, PACK], BF16, name="h1_grp", align_bytes=64)
            if vector_cols > 0:
                group_rows(nc.vector.tensor_copy, grouped, hidden, slice(0, vector_cols))
            if vector_cols < width:
                group_rows(nc.scalar.copy, grouped, hidden, slice(vector_cols, width))
            return grouped

        def quantise_hidden(g, first_row, width, grouped):
            cols = slice(first_row, first_row + width)
            nc.vector.quantize_mx(
                out=h1_codes[:, g, cols].bitcast(FP8X4), scales=h1_scales[:, g, cols], in_=grouped[:].rearrange("p c t -> p (c t)")
            )

        def second_product(half, t, bank_set):
            rows = slice(half * HALF + t * P, half * HALF + (t + 1) * P)
            result = w_raw_pool.tile([P, OUT], F32, name="result", tag="w_raw", bufs=W_BUFS)
            for first, last in OUT_BANKS:
                cols = slice(first, last)
                bank = psum.tile([P, last - first], F32, name="out_bank", tag=bank_set)
                for g in range(PASSES2):
                    nc.tensor.matmul_mx(
                        out=bank[:],
                        lhsT=h1_codes[:, g, rows].bitcast(FP8X4),
                        lhsT_scale=h1_scales[:, g, rows],
                        rhs=w2_codes[:, g, cols].bitcast(FP8X4),
                        rhs_scale=w2_scales[:, g, cols],
                        start=(g == 0),
                        stop=(g == PASSES2 - 1),
                    )
                nc.vector.tensor_tensor(out=result[:, cols], in0=bank[:], in1=b2_all[:, cols], op=ALU.add)
            root = result_pool.tile([P, LATENT], F32, name="root")
            nc.scalar.activation(out=root[:], in_=result[:, LATENT:OUT], func=ACT.Sqrt)
            nc.sync.dma_start(out=outputs[1][half, :, t, :], in_=result[:, LATENT:OUT])
            nc.sync.dma_start(out=outputs[0][half, :, t, :], in_=result[:, 0:LATENT])
            return result, root

        def draw_sample(half, t, result, root):
            noise = result_pool.tile([P, LATENT], F32, name="noise")
            product_engine = nc.gpsimd if half == 0 and t < 2 else nc.vector
            product_engine.tensor_tensor(out=noise[:], in0=root[:], in1=eps_all[:, half, t, :], op=ALU.mult)
            sample = result_pool.tile([P, LATENT], F32, name="sample", bufs=SUB)
            sum_engine = nc.vector if half == 1 and t == SUB - 1 else nc.gpsimd
            sum_engine.tensor_tensor(out=sample[:], in0=noise[:], in1=result[:, 0:LATENT], op=ALU.add)
            nc.sync.dma_start(out=outputs[2][half, :, t, :], in_=sample[:])

        waiting = []

        def finish_tile(half, t, bank_set):
            result, root = second_product(half, t, bank_set)
            if waiting:
                draw_sample(*waiting.pop())
            waiting.append((half, t, result, root))

        ones = keep.tile([P, HALF], BF16)
        nc.vector.memset(ones[:], 1.0)
        b1_rows = keep.tile([P, P], BF16)
        nc.vector.memset(b1_rows[:], 0.0)

        x_raw = {}
        w_raw = {}
        x_raw[0, 0] = new_x()
        fill_x(x_raw[0, 0], 0, 0, slice(0, SUB // 2))
        fill_x(x_raw[0, 0], 0, 0, slice(SUB // 2, SUB))
        w_raw[0, 0] = load_w1(0, 0)
        b1_runs = rep_b1.rearrange("(q b t i) -> q t b i", q=PASSES2, t=PACK, i=RUN)
        for q in range(PASSES2):
            nc.sync.dma_start(out=b1_rows[PACK * q : PACK * (q + 1), :].rearrange("t (b i) -> t b i", i=RUN), in_=b1_runs[q])
        x_raw[0, 1] = load_x(0, 1)
        w_raw[0, 1] = load_w1(0, 1)
        w_raw[0, 2] = load_w1(0, 2)
        x_raw[0, 2] = load_x(0, 2)
        w_raw[0, 3] = load_w1(0, 3)
        w_raw[0, 4] = load_w1(0, 4)
        x_raw[1, 0] = load_x(1, 0)
        w_raw[0, 5] = load_w1(0, 5)
        w_raw[1, 0] = load_w1(1, 0)
        x_raw[1, 1] = load_x(1, 1)
        w_raw[1, 1] = load_w1(1, 1)
        x_raw[1, 2] = load_x(1, 2)
        w_raw[1, 2] = load_w1(1, 2)
        w_raw[1, 3] = load_w1(1, 3)
        w_raw[1, 4] = load_w1(1, 4)
        w_raw[1, 5] = load_w1(1, 5)
        w2_raw = [load_w2(0), load_w2(1)]
        b2_all = keep.tile([P, OUT], BF16)
        nc.sync.dma_start(out=b2_all[:], in_=rep_b2.partition_broadcast(P))
        eps_all = keep.tile([P, HALVES, SUB, LATENT], BF16)
        nc.sync.dma_start(out=eps_all[:], in_=eps.rearrange("(h p t) c -> p h t c", h=HALVES, t=SUB))

        ident = keep.tile([P, P], F32)
        make_identity(nc, ident[:])
        one = keep.tile([P, 1], F32)
        nc.vector.memset(one[:], 1.0)
        one_root = keep.tile([P, 1], F32)
        nc.scalar.activation(out=one_root[:], in_=one[:], func=ACT.Sqrt)

        whole = slice(0, HALF)
        acc = {}
        grouped_w = {}

        grouped_x = {}

        def x_ready(half, chunk):
            quantise_x(half, 2 * chunk, grouped_x[half, chunk][0])
            quantise_x(half, 2 * chunk + 1, grouped_x[half, chunk][1])

        def weight_pass(q, g, vector_tiles=2):
            grouped_w[q, g] = group_w1(w_raw[q, g], vector_tiles)

        def weight_ready(q, g):
            cols = slice(q * K_PASS, (q + 1) * K_PASS)
            nc.vector.quantize_mx(
                out=w1_codes[:, g, cols].bitcast(FP8X4),
                scales=w1_scales[:, g, cols],
                in_=grouped_w[q, g][:].rearrange("p w t -> p (w t)"),
            )

        def turn(half, chunk, pair, engines):
            if pair == 0:
                grouped_x[half, chunk] = new_grouped()
            banks = transpose_pair(x_raw[half, chunk], pair, "x")
            copy_pair(grouped_x[half, chunk], banks, pair, engines)

        def keep_busy(count):
            idle = psum.tile([P, HALF], F32, name="idle", tag="y")
            for n in range(count):
                nc.tensor.matmul(out=idle[:], lhsT=ones[:, 0:P], rhs=ones[:], start=True, stop=True)

        def quantise_w2(g):
            for first, last in OUT_BANKS:
                quantise_weight(w2_codes[:, g, :], w2_scales[:, g, :], grouped_w[g], slice(first, last))

        scalar_both = (nc.scalar.copy, nc.scalar.copy)
        shared = (nc.scalar.copy, nc.vector.tensor_copy)

        keep_busy(6)
        turn(0, 0, 0, shared)
        turn(0, 0, 1, shared)
        weight_pass(0, 0, 2)
        keep_busy(6)
        b1_rows_f32 = keep.tile([P, P], F32)
        nc.vector.tensor_copy(out=b1_rows_f32[:], in_=b1_rows[:])
        b1_bank = psum.tile([P, P], F32, name="b1_bank", tag="y")
        nc.tensor.transpose(out=b1_bank[:], in_=b1_rows_f32[:], identity=ident[:])
        b1_col = keep.tile([P, H_TILES], F32)
        nc.vector.tensor_copy(out=b1_col[:], in_=b1_bank[:, 0:H_TILES])
        x_ready(0, 0)
        weight_ready(0, 0)
        weight_pass(0, 1, 2)
        turn(0, 1, 0, scalar_both)
        turn(0, 1, 1, shared)
        weight_ready(0, 1)
        weight_pass(0, 2, 2)
        open_groups(LOW, "y", HALF)
        first_product(0, LOW, (0, 1,), whole)
        x_ready(0, 1)
        weight_ready(0, 2)
        weight_pass(0, 3, 2)
        turn(0, 2, 0, scalar_both)
        turn(0, 2, 1, shared)
        weight_ready(0, 3)
        weight_pass(0, 4, 2)
        first_product(0, LOW, (2, 3,), whole)
        x_ready(0, 2)
        weight_ready(0, 4)
        weight_pass(0, 5, 2)
        turn(1, 0, 0, scalar_both)
        turn(1, 0, 1, shared)
        weight_ready(0, 5)
        first_product(0, LOW, (4, 5,), whole)
        weight_pass(1, 0, 2)
        x_ready(1, 0)
        weight_ready(1, 0)
        hidden_low = leave_psum(LOW, (1,))
        turn(1, 1, 0, scalar_both)
        turn(1, 1, 1, shared)
        weight_pass(1, 1, 2)
        open_groups(LOW, "y", HALF)
        first_product(1, LOW, (0, 1,), whole)
        x_ready(1, 1)
        weight_ready(1, 1)
        turn(1, 2, 0, scalar_both)
        turn(1, 2, 1, shared)
        weight_pass(1, 2, 2)
        first_product(1, LOW, (2, 3,), whole)
        x_ready(1, 2)
        weight_ready(1, 2)
        weight_pass(1, 3, 2)
        weight_ready(1, 3)

        open_groups(HIGH, "x", HALF)
        first_product(0, HIGH, (0,), whole)
        first_product(1, LOW, (4, 5), whole)
        weight_pass(1, 4, 2)
        grouped_h = group_hidden(hidden_low, HALF, HALF)
        weight_ready(1, 4)
        weight_pass(1, 5, 2)
        quantise_hidden(0, 0, HALF, grouped_h)
        weight_ready(1, 5)
        first_product(0, HIGH, (1, 2, 3, 4, 5), whole)
        hidden_low = leave_psum(LOW, ())
        for g in range(PASSES2):
            grouped_w[g] = group_w2(w2_raw[g])
        quantise_w2(0)
        hidden_high = leave_psum(HIGH, (5,))
        grouped_h = group_hidden(hidden_high, HALF, 384)
        quantise_w2(1)
        quantise_hidden(1, 0, HALF, grouped_h)

        def last_tiles(hidden, quarter, h_tiles, bank_set):
            for h in h_tiles:
                open_groups((h,), bank_set, QUARTER)
                first_product(1, (h,), range(PASSES1), slice(quarter * QUARTER, (quarter + 1) * QUARTER))
                relu_out(hidden, h, False)

        def last_hidden(quarter, hidden, vector_cols):
            grouped = group_hidden(hidden, QUARTER, vector_cols)
            quantise_hidden(1, HALF + quarter * QUARTER, QUARTER, grouped)

        hidden_q = []
        for quarter in range(2):
            hidden_q.append(hidden_pool.tile([P, PACK, QUARTER], BF16, name="hidden_q"))
        last_tiles(hidden_q[0], 0, HIGH[0:4], "y")
        grouped_l = group_hidden(hidden_low, HALF, HALF)
        last_hidden(0, hidden_q[0], 0)
        last_tiles(hidden_q[1], 1, HIGH[0:2], "y")
        finish_tile(0, 0, "x")
        quantise_hidden(0, HALF, HALF, grouped_l)
        finish_tile(0, 1, "x")
        last_tiles(hidden_q[1], 1, HIGH[2:4], "y")
        finish_tile(0, 2, "x")
        finish_tile(0, 3, "x")
        last_hidden(1, hidden_q[1], 128)
        finish_tile(1, 0, "x")
        finish_tile(1, 1, "x")
        finish_tile(1, 2, "x")
        finish_tile(1, 3, "x")
        draw_sample(*waiting.pop())
